import numpy as np
import ml_dtypes


def mxq(x, axis, fmt="e4m3"):
    dtype, down = {"e4m3": (ml_dtypes.float8_e4m3fn, 7), "e5m2": (ml_dtypes.float8_e5m2, 14)}[fmt]
    v = np.moveaxis(np.asarray(x, np.float32).astype(ml_dtypes.bfloat16).astype(np.float64), axis, -1)
    blocks = v.reshape(v.shape[:-1] + (-1, 32))
    amax = np.abs(blocks).max(-1, keepdims=True)
    byte = np.maximum(np.where(amax > 0, np.frexp(amax)[1] - 1 + 127, 0) - down, 1)
    scale = np.exp2(byte - 127.0)
    codes = (blocks / scale).astype(np.float32).astype(dtype).astype(np.float64)
    return np.moveaxis((codes * scale).reshape(v.shape), -1, axis)


WIDE = False


def mx_kscale(k):
    if not WIDE:
        return np.ones(k)
    levels = np.array([10, -10, 5, -5, 0])
    a = np.random.permutation(np.resize(levels, k // 512 * 4)).reshape(k // 512, 4)
    idx = np.arange(k)
    return np.exp2(a[idx // 512, idx % 128 // 32])


BF16 = ml_dtypes.bfloat16


def bf(x):
    return np.asarray(x, np.float32).astype(BF16)


def f64(x):
    return np.asarray(x).astype(np.float64)


B, H, V, DEPTH = 16, 1024, 8192, 5
NODES = 2 ** (DEPTH - 2)
G = 3 * H


def sigmoid(v):
    return 1.0 / (1.0 + np.exp(-v))


def gate(x, g, bih):
    r = sigmoid(g[..., :H] + bih[:H])
    z = sigmoid(g[..., H:2 * H] + bih[H:2 * H])
    n = np.tanh(bih[2 * H:] + r * g[..., 2 * H:])
    return (1.0 - z) * n + z * x


def expand(x, wl, bil, bhl, wr, bir, bhr):
    xq = mxq(x, 2, "e4m3")
    xl = gate(x, (xq @ wl.T) + bhl, bil)
    xr = gate(x, (xq @ wr.T) + bhr, bir)
    return np.stack([xl, xr], axis=2).reshape(B, -1, H)


def setup_inputs():
    w = 1.5 / np.sqrt(H)
    s = mx_kscale(H)
    t = s / s.min()
    return {"h_nodes": bf(np.random.standard_normal((B, NODES, H)) * 0.4 * t),
            "Whh_l": bf(np.random.standard_normal((G, H)) * w / t[None, :]),
            "bih_l": bf(np.random.standard_normal(G) * 0.4),
            "bhh_l": bf(np.random.standard_normal(G) * 0.4),
            "Whh_r": bf(np.random.standard_normal((G, H)) * w / t[None, :]),
            "bih_r": bf(np.random.standard_normal(G) * 0.4),
            "bhh_r": bf(np.random.standard_normal(G) * 0.4)}


def reference(h_nodes, Whh_l, bih_l, bhh_l, Whh_r, bih_r, bhh_r):
    wl = mxq(f64(Whh_l), 1, "e4m3")
    wr = mxq(f64(Whh_r), 1, "e4m3")
    args = (wl, f64(bih_l), f64(bhh_l), wr, f64(bih_r), f64(bhh_r))
    c = expand(f64(h_nodes), *args)
    return expand(c, *args)

@@ -1,0 +1,249 @@
+import concourse.mybir as mybir
+from concourse.masks import make_identity
+
+F32 = mybir.dt.float32
+BF16 = mybir.dt.bfloat16
+U32 = mybir.dt.uint32
+U8 = mybir.dt.uint8
+FP8X4 = mybir.dt.float8_e4m3fn_x4
+ACT = mybir.ActivationFunctionType
+ALU = mybir.AluOpType
+
+P = 128
+H = 1024
+GATES = 3
+SIDES = 2
+PAIR = 2
+ROOTS = 128
+BLOCK = P * PAIR
+BLOCKS = H // BLOCK
+PASSES = H // (4 * P)
+WORD_BLOCKS = H // BLOCK
+BANK = 512
+SLABS = SIDES * BLOCKS * GATES
+SLAB_WORDS = PAIR * PASSES * P
+
+FLOPS = 2 * (ROOTS + SIDES * ROOTS) * (SIDES * GATES * H) * H
+
+
+def tile_decodertreernn_pa_kernel(
+    tc, h_nodes, Whh_l, bih_l, bhh_l, Whh_r, bih_r, bhh_r, out
+):
+    nc = tc.nc
+
+    slab_rows = [
+        w.rearrange("(gate blk q e) k -> gate blk q (e k)", gate=GATES, blk=BLOCKS, q=P, e=PAIR)
+        for w in (Whh_l, Whh_r)
+    ]
+    out_rows = out.rearrange("b (i s s2) h -> (b i) s s2 h", s=SIDES, s2=SIDES)
+
+    def slab_index(side, blk, gate):
+        return (side * BLOCKS + blk) * GATES + gate
+
+    with tc.tile_pool(name="keep", bufs=1) as keep:
+        identity = keep.tile([P, P], F32)
+        make_identity(nc, identity[:])
+
+        w_codes = keep.tile([P, SLABS, SLAB_WORDS], U32, align_bytes=64)
+        w_scales = keep.tile([P, SLABS, SLAB_WORDS], U8, align_bytes=64)
+        x_codes = keep.tile([P, PASSES, ROOTS], U32, align_bytes=64)
+        x_scales = keep.tile([P, PASSES, ROOTS], U8, align_bytes=64)
+        c_codes = keep.tile([P, PASSES, SIDES * ROOTS], U32, align_bytes=64)
+        c_scales = keep.tile([P, PASSES, SIDES * ROOTS], U8, align_bytes=64)
+        x_f32 = keep.tile([P, BLOCKS, PAIR, ROOTS], F32)
+        c_f32 = keep.tile([P, BLOCKS, PAIR, SIDES * ROOTS], F32)
+        c_grouped = keep.tile([P, PASSES, SIDES * ROOTS, 2 * PAIR], BF16, align_bytes=64)
+        bias = keep.tile([P, SIDES * 2 * GATES * BLOCKS * PAIR], F32)
+        bias_rz = keep.tile([P, SIDES, 2 * BLOCKS * PAIR], F32)
+
+        def bias_column(side, kind, gate, blk, e):
+            col = ((side * 2 + kind) * GATES * BLOCKS + gate * BLOCKS + blk) * PAIR + e
+            return bias[:, col : col + 1]
+
+        def bias_rz_column(side, gate, blk, e):
+            col = (gate * BLOCKS + blk) * PAIR + e
+            return bias_rz[:, side, col : col + 1]
+
+        def gru_block(side, blk, codes, scales, nodes, prev, new, gate_psum, work):
+            sums = []
+            for gate in range(GATES):
+                bank = gate_psum.tile([P, PAIR, nodes], F32, name="sums%d" % gate)
+                slab = slab_index(side, blk, gate)
+                for e in range(PAIR):
+                    for g in range(PASSES):
+                        first = (e * PASSES + g) * P
+                        nc.tensor.matmul_mx(
+                            out=bank[:, e, :],
+                            lhsT=w_codes[:, slab, first : first + P].bitcast(FP8X4),
+                            lhsT_scale=w_scales[:, slab, first : first + P],
+                            rhs=codes[:, g, :].bitcast(FP8X4),
+                            rhs_scale=scales[:, g, :],
+                            start=(g == 0),
+                            stop=(g == PASSES - 1),
+                        )
+                sums.append(bank)
+
+            reset = work.tile([P, PAIR, nodes], F32)
+            update = work.tile([P, PAIR, nodes], F32)
+            cand = work.tile([P, PAIR, nodes], F32)
+            diff = work.tile([P, PAIR, nodes], F32)
+            for e in range(PAIR):
+                nc.scalar.activation(
+                    out=reset[:, e, :], in_=sums[0][:, e, :], func=ACT.Sigmoid,
+                    bias=bias_rz_column(side, 0, blk, e), scale=1.0,
+                )
+            for e in range(PAIR):
+                nc.scalar.activation(
+                    out=update[:, e, :], in_=sums[1][:, e, :], func=ACT.Sigmoid,
+                    bias=bias_rz_column(side, 1, blk, e), scale=1.0,
+                )
+            for e in range(PAIR):
+                nc.vector.scalar_tensor_tensor(
+                    out=cand[:, e, :], in0=sums[2][:, e, :], scalar=bias_column(side, 1, 2, blk, e),
+                    in1=reset[:, e, :], op0=ALU.add, op1=ALU.mult,
+                )
+            for e in range(PAIR):
+                nc.scalar.activation(
+                    out=cand[:, e, :], in_=cand[:, e, :], func=ACT.Tanh,
+                    bias=bias_column(side, 0, 2, blk, e), scale=1.0,
+                )
+            nc.vector.tensor_sub(out=diff[:], in0=prev, in1=cand[:])
+            nc.vector.tensor_mul(out=diff[:], in0=update[:], in1=diff[:])
+            nc.vector.tensor_add(out=new, in0=diff[:], in1=cand[:])
+
+        with tc.tile_pool(name="raw", bufs=SLABS) as raw_pool, tc.tile_pool(
+            name="once", bufs=1
+        ) as once, tc.tile_pool(name="stage", bufs=4) as stage, tc.tile_pool(
+            name="work1", bufs=3
+        ) as work1, tc.psum_pool(name="flip", bufs=5) as flip_psum, tc.psum_pool(
+            name="gates1", bufs=1
+        ) as gates1:
+            warm = once.tile([P, 1], F32)
+            nc.vector.memset(warm[:], 0.0)
+            nc.scalar.activation(out=warm[:], in_=warm[:], func=ACT.Sigmoid)
+
+            x_raw = once.tile([P, H], BF16)
+            nc.sync.dma_start(out=x_raw[:], in_=h_nodes.flatten_outer_dims())
+            bias_raw = once.tile([P, BLOCK], BF16)
+            nc.vector.memset(bias_raw[:], 0.0)
+            for v, vec in enumerate((bih_l, bhh_l, bih_r, bhh_r)):
+                rows = GATES * BLOCKS
+                nc.scalar.dma_start(
+                    out=bias_raw[v * rows : (v + 1) * rows, :],
+                    in_=vec.rearrange("(r c) -> r c", c=BLOCK),
+                )
+            blocks = [(blk, side) for blk in range(BLOCKS) for side in range(SIDES)]
+            raw = {}
+            for blk, side in blocks:
+                for gate in range(GATES):
+                    raw_slab = raw_pool.tile([P, PAIR * H], BF16, name="raw_slab")
+                    nc.sync.dma_start(out=raw_slab[:], in_=slab_rows[side][gate, blk])
+                    raw[(side, blk, gate)] = raw_slab
+
+            x_words = x_raw[:].bitcast(F32)
+            x_flipped = flip_psum.tile([P, BANK], F32, name="flipped")
+            for w in range(WORD_BLOCKS):
+                nc.tensor.transpose(
+                    x_flipped[:, w * P : (w + 1) * P], x_words[:, w * P : (w + 1) * P], identity[:]
+                )
+            x_grouped = once.tile([P, BANK], F32, align_bytes=64)
+            nc.vector.tensor_copy(
+                out=x_grouped[:].rearrange("p (g j u) -> p g j u", g=PASSES, u=PAIR),
+                in_=x_flipped[:].rearrange("p (g u j) -> p g j u", g=PASSES, u=PAIR),
+            )
+            nc.scalar.copy(
+                out=x_f32[:],
+                in_=x_flipped[:].bitcast(BF16).rearrange(
+                    "p (blk j e) -> p blk e j", blk=BLOCKS, e=PAIR
+                ),
+            )
+            nc.vector.quantize_mx(
+                out=x_codes[:].rearrange("p g j -> p (g j)").bitcast(FP8X4),
+                scales=x_scales[:].rearrange("p g j -> p (g j)"),
+                in_=x_grouped[:].bitcast(BF16),
+            )
+
+            b_flipped = flip_psum.tile([P, BANK], F32, name="flipped")
+            nc.tensor.transpose(b_flipped[:, 0:P], bias_raw[:].bitcast(F32), identity[:])
+            bias_words = SIDES * 2 * GATES * BLOCKS
+            nc.vector.tensor_copy(out=bias[:], in_=b_flipped[:, 0:bias_words].bitcast(BF16))
+            by_kind = bias[:].rearrange("p (s kind c) -> p s kind c", s=SIDES, kind=2)
+            rz_cols = 2 * BLOCKS * PAIR
+            nc.vector.tensor_add(
+                out=bias_rz[:], in0=by_kind[:, :, 0, 0:rz_cols], in1=by_kind[:, :, 1, 0:rz_cols]
+            )
+
+            def quantise_slab(side, blk, gate):
+                words = raw[(side, blk, gate)][:].bitcast(F32)
+                grouped = stage.tile([P, PAIR * BANK], F32, align_bytes=64)
+                for e in range(PAIR):
+                    flipped = flip_psum.tile([P, BANK], F32, name="flipped")
+                    for w in range(WORD_BLOCKS):
+                        first = (e * WORD_BLOCKS + w) * P
+                        nc.tensor.transpose(
+                            flipped[:, w * P : (w + 1) * P], words[:, first : first + P], identity[:]
+                        )
+                    copy = nc.vector.tensor_copy if (gate == GATES - 1 and e == 1) else nc.scalar.copy
+                    copy(
+                        out=grouped[:, e * BANK : (e + 1) * BANK].rearrange(
+                            "p (g q u) -> p g q u", g=PASSES, u=PAIR
+                        ),
+                        in_=flipped[:].rearrange("p (g u q) -> p g q u", g=PASSES, u=PAIR),
+                    )
+                slab = slab_index(side, blk, gate)
+                nc.vector.quantize_mx(
+                    out=w_codes[:, slab, :].bitcast(FP8X4),
+                    scales=w_scales[:, slab, :],
+                    in_=grouped[:].bitcast(BF16),
+                )
+
+            def first_level(blk, side):
+                nodes = slice(side * ROOTS, (side + 1) * ROOTS)
+                gru_block(
+                    side, blk, x_codes, x_scales, ROOTS,
+                    x_f32[:, blk, :, :], c_f32[:, blk, :, nodes], gates1, work1,
+                )
+                g, u = divmod(blk, PAIR)
+                nc.vector.tensor_copy(
+                    out=c_grouped[:, g, nodes, u * PAIR : (u + 1) * PAIR],
+                    in_=c_f32[:, blk, :, nodes].rearrange("p e j -> p j e"),
+                )
+                if u == PAIR - 1 and side == SIDES - 1:
+                    nc.vector.quantize_mx(
+                        out=c_codes[:, g, :].bitcast(FP8X4),
+                        scales=c_scales[:, g, :],
+                        in_=c_grouped[:, g, :, :].rearrange("p c t -> p (c t)"),
+                    )
+
+            for i, (blk, side) in enumerate(blocks):
+                for gate in range(GATES):
+                    quantise_slab(side, blk, gate)
+                if i > 0:
+                    first_level(*blocks[i - 1])
+            first_level(*blocks[-1])
+
+        with tc.tile_pool(name="work2", bufs=3) as work2, tc.tile_pool(
+            name="result", bufs=1
+        ) as result, tc.psum_pool(name="gates2", bufs=2) as gates2, tc.psum_pool(
+            name="back", bufs=2
+        ) as back_psum:
+            out_sb = result.tile([P, SIDES, SIDES, H], F32)
+            for side2 in range(SIDES):
+                for blk in range(BLOCKS):
+                    mixed = work2.tile([P, PAIR, SIDES * ROOTS], F32)
+                    gru_block(
+                        side2, blk, c_codes, c_scales, SIDES * ROOTS,
+                        c_f32[:, blk, :, :], mixed[:], gates2, work2,
+                    )
+                    back = back_psum.tile([P, SIDES, PAIR, P], F32)
+                    for s in range(SIDES):
+                        for e in range(PAIR):
+                            nc.tensor.transpose(
+                                back[:, s, e, :], mixed[:, e, s * ROOTS : (s + 1) * ROOTS], identity[:]
+                            )
+                    cols = slice(blk * BLOCK, (blk + 1) * BLOCK)
+                    nc.scalar.copy(
+                        out=out_sb[:, :, side2, cols].rearrange("j s (q e) -> j s q e", e=PAIR),
+                        in_=back[:].rearrange("j s e q -> j s q e"),
+                    )
+                    nc.sync.dma_start(out=out_rows[:, :, side2, cols], in_=out_sb[:, :, side2, cols])

@@ -23,6 +23,12 @@ BANK = 512
 SLABS = SIDES * BLOCKS * GATES
 SLAB_WORDS = PAIR * PASSES * P
 
+MULTIPLY_LAG = 3
+TANH_LAG = 6
+MIX_LAG = 7
+CAST_LAG = 8
+WARM_UP = 6
+
 FLOPS = 2 * (ROOTS + SIDES * ROOTS) * (SIDES * GATES * H) * H
 
 
@@ -37,10 +43,17 @@ def tile_decodertreernn_pa_kernel(
     ]
     out_rows = out.rearrange("b (i s s2) h -> (b i) s s2 h", s=SIDES, s2=SIDES)
 
-    def slab_index(side, blk, gate):
-        return (side * BLOCKS + blk) * GATES + gate
+    slabs = [
+        (blk, side, gate)
+        for blk in range(BLOCKS)
+        for side in range(SIDES)
+        for gate in range(GATES)
+    ]
 
-    with tc.tile_pool(name="keep", bufs=1) as keep:
+    def slab_index(blk, side, gate):
+        return (blk * SIDES + side) * GATES + gate
+
+    with tc.manual_schedule(), tc.tile_pool(name="keep", bufs=1) as keep:
         identity = keep.tile([P, P], F32)
         make_identity(nc, identity[:])
 
@@ -64,66 +77,57 @@ def tile_decodertreernn_pa_kernel(
             col = (gate * BLOCKS + blk) * PAIR + e
             return bias_rz[:, side, col : col + 1]
 
-        def gru_block(side, blk, codes, scales, nodes, prev, new, gate_psum, work):
-            sums = []
-            for gate in range(GATES):
-                bank = gate_psum.tile([P, PAIR, nodes], F32, name="sums%d" % gate)
-                slab = slab_index(side, blk, gate)
-                for e in range(PAIR):
-                    for g in range(PASSES):
-                        first = (e * PASSES + g) * P
-                        nc.tensor.matmul_mx(
-                            out=bank[:, e, :],
-                            lhsT=w_codes[:, slab, first : first + P].bitcast(FP8X4),
-                            lhsT_scale=w_scales[:, slab, first : first + P],
-                            rhs=codes[:, g, :].bitcast(FP8X4),
-                            rhs_scale=scales[:, g, :],
-                            start=(g == 0),
-                            stop=(g == PASSES - 1),
-                        )
-                sums.append(bank)
+        def multiply(bank, slab, codes, scales):
+            for e in range(PAIR):
+                for g in range(PASSES):
+                    first = (e * PASSES + g) * P
+                    nc.tensor.matmul_mx(
+                        out=bank[:, e, :],
+                        lhsT=w_codes[:, slab, first : first + P].bitcast(FP8X4),
+                        lhsT_scale=w_scales[:, slab, first : first + P],
+                        rhs=codes[:, g, :].bitcast(FP8X4),
+                        rhs_scale=scales[:, g, :],
+                        start=(g == 0),
+                        stop=(g == PASSES - 1),
+                    )
 
-            reset = work.tile([P, PAIR, nodes], F32)
-            update = work.tile([P, PAIR, nodes], F32)
-            cand = work.tile([P, PAIR, nodes], F32)
-            diff = work.tile([P, PAIR, nodes], F32)
-            for e in range(PAIR):
-                nc.scalar.activation(
-                    out=reset[:, e, :], in_=sums[0][:, e, :], func=ACT.Sigmoid,
-                    bias=bias_rz_column(side, 0, blk, e), scale=1.0,
-                )
-            for e in range(PAIR):
-                nc.scalar.activation(
-                    out=update[:, e, :], in_=sums[1][:, e, :], func=ACT.Sigmoid,
-                    bias=bias_rz_column(side, 1, blk, e), scale=1.0,
-                )
+        def sigmoid(gate_out, bank, side, gate, blk, e):
+            nc.scalar.activation(
+                out=gate_out[:, e, :], in_=bank[:, e, :], func=ACT.Sigmoid,
+                bias=bias_rz_column(side, gate, blk, e), scale=1.0,
+            )
+
+        def reset_candidate(cand, bank, reset, side, blk):
             for e in range(PAIR):
                 nc.vector.scalar_tensor_tensor(
-                    out=cand[:, e, :], in0=sums[2][:, e, :], scalar=bias_column(side, 1, 2, blk, e),
+                    out=cand[:, e, :], in0=bank[:, e, :], scalar=bias_column(side, 1, 2, blk, e),
                     in1=reset[:, e, :], op0=ALU.add, op1=ALU.mult,
                 )
-            for e in range(PAIR):
-                nc.scalar.activation(
-                    out=cand[:, e, :], in_=cand[:, e, :], func=ACT.Tanh,
-                    bias=bias_column(side, 0, 2, blk, e), scale=1.0,
-                )
+
+        def tanh(cand, side, blk, e):
+            nc.scalar.activation(
+                out=cand[:, e, :], in_=cand[:, e, :], func=ACT.Tanh,
+                bias=bias_column(side, 0, 2, blk, e), scale=1.0,
+            )
+
+        def mix_begin(diff, prev, cand, update):
             nc.vector.tensor_sub(out=diff[:], in0=prev, in1=cand[:])
             nc.vector.tensor_mul(out=diff[:], in0=update[:], in1=diff[:])
-            nc.vector.tensor_add(out=new, in0=diff[:], in1=cand[:])
 
         with tc.tile_pool(name="raw", bufs=SLABS) as raw_pool, tc.tile_pool(
             name="once", bufs=1
         ) as once, tc.tile_pool(name="stage", bufs=4) as stage, tc.tile_pool(
             name="work1", bufs=3
         ) as work1, tc.psum_pool(name="flip", bufs=5) as flip_psum, tc.psum_pool(
-            name="gates1", bufs=1
+            name="gates1", bufs=3
         ) as gates1:
-            warm = once.tile([P, 1], F32)
-            nc.vector.memset(warm[:], 0.0)
-            nc.scalar.activation(out=warm[:], in_=warm[:], func=ACT.Sigmoid)
-
             x_raw = once.tile([P, H], BF16)
             nc.sync.dma_start(out=x_raw[:], in_=h_nodes.flatten_outer_dims())
+            raw = []
+            for blk, side, gate in slabs:
+                raw_slab = raw_pool.tile([P, PAIR * H], BF16, name="raw_slab")
+                nc.sync.dma_start(out=raw_slab[:], in_=slab_rows[side][gate, blk])
+                raw.append(raw_slab)
             bias_raw = once.tile([P, BLOCK], BF16)
             nc.vector.memset(bias_raw[:], 0.0)
             for v, vec in enumerate((bih_l, bhh_l, bih_r, bhh_r)):
@@ -132,13 +136,22 @@ def tile_decodertreernn_pa_kernel(
                     out=bias_raw[v * rows : (v + 1) * rows, :],
                     in_=vec.rearrange("(r c) -> r c", c=BLOCK),
                 )
-            blocks = [(blk, side) for blk in range(BLOCKS) for side in range(SIDES)]
-            raw = {}
-            for blk, side in blocks:
-                for gate in range(GATES):
-                    raw_slab = raw_pool.tile([P, PAIR * H], BF16, name="raw_slab")
-                    nc.sync.dma_start(out=raw_slab[:], in_=slab_rows[side][gate, blk])
-                    raw[(side, blk, gate)] = raw_slab
+
+            warm = once.tile([P, 1], F32)
+            nc.vector.memset(warm[:], 0.0)
+            nc.scalar.activation(out=warm[:], in_=warm[:], func=ACT.Sigmoid)
+
+            zeros = once.tile([P, BANK], BF16)
+            nc.vector.memset(zeros[:], 0.0)
+
+            def idle_matmuls(count):
+                unread = gates1.tile([P, BANK], F32, name="sums")
+                for i in range(count):
+                    nc.tensor.matmul(
+                        out=unread[:], lhsT=zeros[:, 0:P], rhs=zeros[:], start=True, stop=True
+                    )
+
+            idle_matmuls(WARM_UP)
 
             x_words = x_raw[:].bitcast(F32)
             x_flipped = flip_psum.tile([P, BANK], F32, name="flipped")
@@ -157,11 +170,6 @@ def tile_decodertreernn_pa_kernel(
                     "p (blk j e) -> p blk e j", blk=BLOCKS, e=PAIR
                 ),
             )
-            nc.vector.quantize_mx(
-                out=x_codes[:].rearrange("p g j -> p (g j)").bitcast(FP8X4),
-                scales=x_scales[:].rearrange("p g j -> p (g j)"),
-                in_=x_grouped[:].bitcast(BF16),
-            )
 
             b_flipped = flip_psum.tile([P, BANK], F32, name="flipped")
             nc.tensor.transpose(b_flipped[:, 0:P], bias_raw[:].bitcast(F32), identity[:])
@@ -172,55 +180,110 @@ def tile_decodertreernn_pa_kernel(
             nc.vector.tensor_add(
                 out=bias_rz[:], in0=by_kind[:, :, 0, 0:rz_cols], in1=by_kind[:, :, 1, 0:rz_cols]
             )
+            nc.vector.quantize_mx(
+                out=x_codes[:].rearrange("p g j -> p (g j)").bitcast(FP8X4),
+                scales=x_scales[:].rearrange("p g j -> p (g j)"),
+                in_=x_grouped[:].bitcast(BF16),
+            )
 
-            def quantise_slab(side, blk, gate):
-                words = raw[(side, blk, gate)][:].bitcast(F32)
-                grouped = stage.tile([P, PAIR * BANK], F32, align_bytes=64)
+            flipped = {}
+            grouped = {}
+            sums = {}
+            reset, update, cand, diff = {}, {}, {}, {}
+
+            def transpose_slab(n):
+                words = raw[n][:].bitcast(F32)
                 for e in range(PAIR):
-                    flipped = flip_psum.tile([P, BANK], F32, name="flipped")
+                    flipped[(n, e)] = flip_psum.tile([P, BANK], F32, name="flipped")
                     for w in range(WORD_BLOCKS):
                         first = (e * WORD_BLOCKS + w) * P
                         nc.tensor.transpose(
-                            flipped[:, w * P : (w + 1) * P], words[:, first : first + P], identity[:]
+                            flipped[(n, e)][:, w * P : (w + 1) * P],
+                            words[:, first : first + P],
+                            identity[:],
                         )
-                    copy = nc.vector.tensor_copy if (gate == GATES - 1 and e == 1) else nc.scalar.copy
-                    copy(
-                        out=grouped[:, e * BANK : (e + 1) * BANK].rearrange(
-                            "p (g q u) -> p g q u", g=PASSES, u=PAIR
-                        ),
-                        in_=flipped[:].rearrange("p (g u q) -> p g q u", g=PASSES, u=PAIR),
-                    )
-                slab = slab_index(side, blk, gate)
+
+            def empty_bank(n, e):
+                if e == 0:
+                    grouped[n] = stage.tile([P, PAIR * BANK], F32, align_bytes=64, name="grouped")
+                by_vector = n % GATES == GATES - 1 and e == PAIR - 1
+                copy = nc.vector.tensor_copy if by_vector else nc.scalar.copy
+                copy(
+                    out=grouped[n][:, e * BANK : (e + 1) * BANK].rearrange(
+                        "p (g q u) -> p g q u", g=PASSES, u=PAIR
+                    ),
+                    in_=flipped[(n, e)][:].rearrange("p (g u q) -> p g q u", g=PASSES, u=PAIR),
+                )
+
+            def quantise_slab(n):
                 nc.vector.quantize_mx(
-                    out=w_codes[:, slab, :].bitcast(FP8X4),
-                    scales=w_scales[:, slab, :],
-                    in_=grouped[:].bitcast(BF16),
+                    out=w_codes[:, n, :].bitcast(FP8X4),
+                    scales=w_scales[:, n, :],
+                    in_=grouped[n][:].bitcast(BF16),
                 )
 
-            def first_level(blk, side):
+            def multiply_slab(n):
+                sums[n] = gates1.tile([P, PAIR, ROOTS], F32, name="sums")
+                multiply(sums[n], n, x_codes, x_scales)
+
+            def activate(n, e):
+                m = n - MULTIPLY_LAG
+                if n % GATES == GATES - 1:
+                    m = n - TANH_LAG
+                if not 0 <= m < SLABS:
+                    return
+                blk, side, gate = slabs[m]
+                i = m // GATES
+                if gate == GATES - 1:
+                    tanh(cand[i], side, blk, e)
+                    return
+                gate_out = (reset, update)[gate]
+                if e == 0:
+                    gate_out[i] = work1.tile([P, PAIR, ROOTS], F32, name=("reset", "update")[gate])
+                sigmoid(gate_out[i], sums[m], side, gate, blk, e)
+
+            def mix(n):
+                lag = (MIX_LAG, CAST_LAG, MULTIPLY_LAG)[n % GATES]
+                m = n - lag
+                if not 0 <= m < SLABS:
+                    return
+                blk, side, gate = slabs[m]
+                i = m // GATES
                 nodes = slice(side * ROOTS, (side + 1) * ROOTS)
-                gru_block(
-                    side, blk, x_codes, x_scales, ROOTS,
-                    x_f32[:, blk, :, :], c_f32[:, blk, :, nodes], gates1, work1,
-                )
-                g, u = divmod(blk, PAIR)
-                nc.vector.tensor_copy(
-                    out=c_grouped[:, g, nodes, u * PAIR : (u + 1) * PAIR],
-                    in_=c_f32[:, blk, :, nodes].rearrange("p e j -> p j e"),
-                )
-                if u == PAIR - 1 and side == SIDES - 1:
-                    nc.vector.quantize_mx(
-                        out=c_codes[:, g, :].bitcast(FP8X4),
-                        scales=c_scales[:, g, :],
-                        in_=c_grouped[:, g, :, :].rearrange("p c t -> p (c t)"),
+                if lag == MULTIPLY_LAG:
+                    cand[i] = work1.tile([P, PAIR, ROOTS], F32, name="cand")
+                    reset_candidate(cand[i], sums[m], reset[i], side, blk)
+                elif lag == MIX_LAG:
+                    diff[i] = work1.tile([P, PAIR, ROOTS], F32, name="diff")
+                    mix_begin(diff[i], x_f32[:, blk, :, :], cand[i], update[i])
+                else:
+                    nc.vector.tensor_add(out=c_f32[:, blk, :, nodes], in0=diff[i][:], in1=cand[i][:])
+                    g, u = divmod(blk, PAIR)
+                    nc.vector.tensor_copy(
+                        out=c_grouped[:, g, nodes, u * PAIR : (u + 1) * PAIR],
+                        in_=c_f32[:, blk, :, nodes].rearrange("p e j -> p j e"),
                     )
+                    if u == PAIR - 1 and side == SIDES - 1:
+                        nc.vector.quantize_mx(
+                            out=c_codes[:, g, :].bitcast(FP8X4),
+                            scales=c_scales[:, g, :],
+                            in_=c_grouped[:, g, :, :].rearrange("p c t -> p (c t)"),
+                        )
 
-            for i, (blk, side) in enumerate(blocks):
-                for gate in range(GATES):
-                    quantise_slab(side, blk, gate)
-                if i > 0:
-                    first_level(*blocks[i - 1])
-            first_level(*blocks[-1])
+            for n in range(SLABS + CAST_LAG + 1):
+                if n < SLABS:
+                    transpose_slab(n)
+                if 0 <= n - MULTIPLY_LAG < SLABS:
+                    multiply_slab(n - MULTIPLY_LAG)
+                else:
+                    idle_matmuls(1)
+                if 0 <= n - 1 < SLABS:
+                    quantise_slab(n - 1)
+                for e in range(PAIR):
+                    if n < SLABS:
+                        empty_bank(n, e)
+                    activate(n, e)
+                mix(n)
 
         with tc.tile_pool(name="work2", bufs=3) as work2, tc.tile_pool(
             name="result", bufs=1
@@ -228,22 +291,63 @@ def tile_decodertreernn_pa_kernel(
             name="back", bufs=2
         ) as back_psum:
             out_sb = result.tile([P, SIDES, SIDES, H], F32)
-            for side2 in range(SIDES):
-                for blk in range(BLOCKS):
-                    mixed = work2.tile([P, PAIR, SIDES * ROOTS], F32)
-                    gru_block(
-                        side2, blk, c_codes, c_scales, SIDES * ROOTS,
-                        c_f32[:, blk, :, :], mixed[:], gates2, work2,
-                    )
-                    back = back_psum.tile([P, SIDES, PAIR, P], F32)
-                    for s in range(SIDES):
-                        for e in range(PAIR):
-                            nc.tensor.transpose(
-                                back[:, s, e, :], mixed[:, e, s * ROOTS : (s + 1) * ROOTS], identity[:]
-                            )
-                    cols = slice(blk * BLOCK, (blk + 1) * BLOCK)
-                    nc.scalar.copy(
-                        out=out_sb[:, :, side2, cols].rearrange("j s (q e) -> j s q e", e=PAIR),
-                        in_=back[:].rearrange("j s e q -> j s q e"),
-                    )
-                    nc.sync.dma_start(out=out_rows[:, :, side2, cols], in_=out_sb[:, :, side2, cols])
+            children = SIDES * ROOTS
+            blocks2 = [(side2, blk) for side2 in range(SIDES) for blk in range(BLOCKS)]
+            update2, cand2, mixed, back = {}, {}, {}, {}
+
+            def gates_of_block(k):
+                side2, blk = blocks2[k]
+                banks = []
+                for gate in range(GATES):
+                    bank = gates2.tile([P, PAIR, children], F32, name="sums%d" % gate)
+                    multiply(bank, slab_index(blk, side2, gate), c_codes, c_scales)
+                    banks.append(bank)
+                return banks
+
+            def activate_block(k, banks):
+                side2, blk = blocks2[k]
+                reset2 = work2.tile([P, PAIR, children], F32)
+                update2[k] = work2.tile([P, PAIR, children], F32, name="update2")
+                cand2[k] = work2.tile([P, PAIR, children], F32, name="cand2")
+                for e in range(PAIR):
+                    sigmoid(reset2, banks[0], side2, 0, blk, e)
+                for e in range(PAIR):
+                    sigmoid(update2[k], banks[1], side2, 1, blk, e)
+                reset_candidate(cand2[k], banks[2], reset2, side2, blk)
+                for e in range(PAIR):
+                    tanh(cand2[k], side2, blk, e)
+
+            def mix_block(k):
+                side2, blk = blocks2[k]
+                mixed[k] = work2.tile([P, PAIR, children], F32, name="mixed")
+                mix_begin(mixed[k], c_f32[:, blk, :, :], cand2[k], update2[k])
+                nc.vector.tensor_add(out=mixed[k][:], in0=mixed[k][:], in1=cand2[k][:])
+
+            def transpose_back(k):
+                back[k] = back_psum.tile([P, SIDES, PAIR, P], F32, name="back")
+                for s in range(SIDES):
+                    for e in range(PAIR):
+                        nc.tensor.transpose(
+                            back[k][:, s, e, :], mixed[k][:, e, s * ROOTS : (s + 1) * ROOTS], identity[:]
+                        )
+
+            def store_block(k):
+                side2, blk = blocks2[k]
+                cols = slice(blk * BLOCK, (blk + 1) * BLOCK)
+                nc.scalar.copy(
+                    out=out_sb[:, :, side2, cols].rearrange("j s (q e) -> j s q e", e=PAIR),
+                    in_=back[k][:].rearrange("j s e q -> j s q e"),
+                )
+                nc.sync.dma_start(out=out_rows[:, :, side2, cols], in_=out_sb[:, :, side2, cols])
+
+            for k in range(len(blocks2) + 2):
+                if k < len(blocks2):
+                    banks = gates_of_block(k)
+                if k >= 2:
+                    transpose_back(k - 2)
+                if k < len(blocks2):
+                    activate_block(k, banks)
+                if k >= 2:
+                    store_block(k - 2)
+                if 1 <= k <= len(blocks2):
+                    mix_block(k - 1)

@@ -57,15 +57,34 @@ def tile_decodertreernn_pa_kernel(
         identity = keep.tile([P, P], F32)
         make_identity(nc, identity[:])
 
-        w_codes = keep.tile([P, SLABS, SLAB_WORDS], U32, align_bytes=64)
-        w_scales = keep.tile([P, SLABS, SLAB_WORDS], U8, align_bytes=64)
-        x_codes = keep.tile([P, PASSES, ROOTS], U32, align_bytes=64)
-        x_scales = keep.tile([P, PASSES, ROOTS], U8, align_bytes=64)
-        c_codes = keep.tile([P, PASSES, SIDES * ROOTS], U32, align_bytes=64)
-        c_scales = keep.tile([P, PASSES, SIDES * ROOTS], U8, align_bytes=64)
+        w_codes = [
+            keep.tile([P, SLAB_WORDS], U32, align_bytes=64, name="w_codes%d" % n) for n in range(SLABS)
+        ]
+        w_scales = [
+            keep.tile([P, SLAB_WORDS], U8, align_bytes=64, name="w_scales%d" % n) for n in range(SLABS)
+        ]
+        x_codes = [
+            keep.tile([P, ROOTS], U32, align_bytes=64, name="x_codes%d" % g) for g in range(PASSES)
+        ]
+        x_scales = [
+            keep.tile([P, ROOTS], U8, align_bytes=64, name="x_scales%d" % g) for g in range(PASSES)
+        ]
+        c_codes = [
+            keep.tile([P, SIDES * ROOTS], U32, align_bytes=64, name="c_codes%d" % g)
+            for g in range(PASSES)
+        ]
+        c_scales = [
+            keep.tile([P, SIDES * ROOTS], U8, align_bytes=64, name="c_scales%d" % g)
+            for g in range(PASSES)
+        ]
         x_f32 = keep.tile([P, BLOCKS, PAIR, ROOTS], F32)
-        c_f32 = keep.tile([P, BLOCKS, PAIR, SIDES * ROOTS], F32)
-        c_grouped = keep.tile([P, PASSES, SIDES * ROOTS, 2 * PAIR], BF16, align_bytes=64)
+        c_f32 = [
+            keep.tile([P, PAIR, SIDES * ROOTS], F32, name="c_f32_%d" % blk) for blk in range(BLOCKS)
+        ]
+        c_grouped = [
+            keep.tile([P, SIDES * ROOTS, 2 * PAIR], BF16, align_bytes=64, name="c_grouped%d" % g)
+            for g in range(PASSES)
+        ]
         bias = keep.tile([P, SIDES * 2 * GATES * BLOCKS * PAIR], F32)
         bias_rz = keep.tile([P, SIDES, 2 * BLOCKS * PAIR], F32)
 
@@ -83,10 +102,10 @@ def tile_decodertreernn_pa_kernel(
                     first = (e * PASSES + g) * P
                     nc.tensor.matmul_mx(
                         out=bank[:, e, :],
-                        lhsT=w_codes[:, slab, first : first + P].bitcast(FP8X4),
-                        lhsT_scale=w_scales[:, slab, first : first + P],
-                        rhs=codes[:, g, :].bitcast(FP8X4),
-                        rhs_scale=scales[:, g, :],
+                        lhsT=w_codes[slab][:, first : first + P].bitcast(FP8X4),
+                        lhsT_scale=w_scales[slab][:, first : first + P],
+                        rhs=codes[g][:].bitcast(FP8X4),
+                        rhs_scale=scales[g][:],
                         start=(g == 0),
                         stop=(g == PASSES - 1),
                     )
@@ -118,9 +137,9 @@ def tile_decodertreernn_pa_kernel(
             name="once", bufs=1
         ) as once, tc.tile_pool(name="stage", bufs=4) as stage, tc.tile_pool(
             name="work1", bufs=3
-        ) as work1, tc.psum_pool(name="flip", bufs=5) as flip_psum, tc.psum_pool(
+        ) as work1, tc.psum_pool(name="flip", bufs=4) as flip_psum, tc.psum_pool(
             name="gates1", bufs=3
-        ) as gates1:
+        ) as gates1, tc.psum_pool(name="idle", bufs=1) as idle_psum:
             x_raw = once.tile([P, H], BF16)
             nc.sync.dma_start(out=x_raw[:], in_=h_nodes.flatten_outer_dims())
             raw = []
@@ -143,13 +162,24 @@ def tile_decodertreernn_pa_kernel(
 
             zeros = once.tile([P, BANK], BF16)
             nc.vector.memset(zeros[:], 0.0)
+            unread = idle_psum.tile([P, BANK], F32)
 
             def idle_matmuls(count):
-                unread = gates1.tile([P, BANK], F32, name="sums")
                 for i in range(count):
                     nc.tensor.matmul(
                         out=unread[:], lhsT=zeros[:, 0:P], rhs=zeros[:], start=True, stop=True
                     )
+
+            def idle_pass(n):
+                nc.tensor.matmul_mx(
+                    out=unread[:],
+                    lhsT=x_codes[0][:].bitcast(FP8X4),
+                    lhsT_scale=x_scales[0][:],
+                    rhs=w_codes[n][:].bitcast(FP8X4),
+                    rhs_scale=w_scales[n][:],
+                    start=True,
+                    stop=True,
+                )
 
             idle_matmuls(WARM_UP)
 
@@ -180,11 +210,12 @@ def tile_decodertreernn_pa_kernel(
             nc.vector.tensor_add(
                 out=bias_rz[:], in0=by_kind[:, :, 0, 0:rz_cols], in1=by_kind[:, :, 1, 0:rz_cols]
             )
-            nc.vector.quantize_mx(
-                out=x_codes[:].rearrange("p g j -> p (g j)").bitcast(FP8X4),
-                scales=x_scales[:].rearrange("p g j -> p (g j)"),
-                in_=x_grouped[:].bitcast(BF16),
-            )
+            for g in range(PASSES):
+                nc.vector.quantize_mx(
+                    out=x_codes[g][:].bitcast(FP8X4),
+                    scales=x_scales[g][:],
+                    in_=x_grouped[:, g * BLOCK : (g + 1) * BLOCK].bitcast(BF16),
+                )
 
             flipped = {}
             grouped = {}
@@ -217,8 +248,8 @@ def tile_decodertreernn_pa_kernel(
 
             def quantise_slab(n):
                 nc.vector.quantize_mx(
-                    out=w_codes[:, n, :].bitcast(FP8X4),
-                    scales=w_scales[:, n, :],
+                    out=w_codes[n][:].bitcast(FP8X4),
+                    scales=w_scales[n][:],
                     in_=grouped[n][:].bitcast(BF16),
                 )
 
@@ -257,26 +288,28 @@ def tile_decodertreernn_pa_kernel(
                     diff[i] = work1.tile([P, PAIR, ROOTS], F32, name="diff")
                     mix_begin(diff[i], x_f32[:, blk, :, :], cand[i], update[i])
                 else:
-                    nc.vector.tensor_add(out=c_f32[:, blk, :, nodes], in0=diff[i][:], in1=cand[i][:])
+                    nc.vector.tensor_add(out=c_f32[blk][:, :, nodes], in0=diff[i][:], in1=cand[i][:])
                     g, u = divmod(blk, PAIR)
                     nc.vector.tensor_copy(
-                        out=c_grouped[:, g, nodes, u * PAIR : (u + 1) * PAIR],
-                        in_=c_f32[:, blk, :, nodes].rearrange("p e j -> p j e"),
+                        out=c_grouped[g][:, nodes, u * PAIR : (u + 1) * PAIR],
+                        in_=c_f32[blk][:, :, nodes].rearrange("p e j -> p j e"),
                     )
                     if u == PAIR - 1 and side == SIDES - 1:
                         nc.vector.quantize_mx(
-                            out=c_codes[:, g, :].bitcast(FP8X4),
-                            scales=c_scales[:, g, :],
-                            in_=c_grouped[:, g, :, :].rearrange("p c t -> p (c t)"),
+                            out=c_codes[g][:].bitcast(FP8X4),
+                            scales=c_scales[g][:],
+                            in_=c_grouped[g][:].rearrange("p c t -> p (c t)"),
                         )
 
             for n in range(SLABS + CAST_LAG + 1):
                 if n < SLABS:
                     transpose_slab(n)
-                if 0 <= n - MULTIPLY_LAG < SLABS:
-                    multiply_slab(n - MULTIPLY_LAG)
-                else:
+                if n < MULTIPLY_LAG:
                     idle_matmuls(1)
+                else:
+                    if n - MULTIPLY_LAG < SLABS:
+                        multiply_slab(n - MULTIPLY_LAG)
+                    idle_pass(min(n - MULTIPLY_LAG, SLABS - 1))
                 if 0 <= n - 1 < SLABS:
                     quantise_slab(n - 1)
                 for e in range(PAIR):
@@ -285,12 +318,9 @@ def tile_decodertreernn_pa_kernel(
                     activate(n, e)
                 mix(n)
 
-        with tc.tile_pool(name="work2", bufs=3) as work2, tc.tile_pool(
-            name="result", bufs=1
-        ) as result, tc.psum_pool(name="gates2", bufs=2) as gates2, tc.psum_pool(
-            name="back", bufs=2
-        ) as back_psum:
-            out_sb = result.tile([P, SIDES, SIDES, H], F32)
+        with tc.tile_pool(name="work2", bufs=3) as work2, tc.psum_pool(
+            name="gates2", bufs=2
+        ) as gates2, tc.psum_pool(name="back", bufs=2) as back_psum:
             children = SIDES * ROOTS
             blocks2 = [(side2, blk) for side2 in range(SIDES) for blk in range(BLOCKS)]
             update2, cand2, mixed, back = {}, {}, {}, {}
@@ -320,7 +350,7 @@ def tile_decodertreernn_pa_kernel(
             def mix_block(k):
                 side2, blk = blocks2[k]
                 mixed[k] = work2.tile([P, PAIR, children], F32, name="mixed")
-                mix_begin(mixed[k], c_f32[:, blk, :, :], cand2[k], update2[k])
+                mix_begin(mixed[k], c_f32[blk][:], cand2[k], update2[k])
                 nc.vector.tensor_add(out=mixed[k][:], in0=mixed[k][:], in1=cand2[k][:])
 
             def transpose_back(k):
@@ -334,11 +364,12 @@ def tile_decodertreernn_pa_kernel(
             def store_block(k):
                 side2, blk = blocks2[k]
                 cols = slice(blk * BLOCK, (blk + 1) * BLOCK)
+                leaving = work2.tile([P, SIDES, BLOCK], F32)
                 nc.scalar.copy(
-                    out=out_sb[:, :, side2, cols].rearrange("j s (q e) -> j s q e", e=PAIR),
+                    out=leaving[:].rearrange("j s (q e) -> j s q e", e=PAIR),
                     in_=back[k][:].rearrange("j s e q -> j s q e"),
                 )
-                nc.sync.dma_start(out=out_rows[:, :, side2, cols], in_=out_sb[:, :, side2, cols])
+                nc.sync.dma_start(out=out_rows[:, :, side2, cols], in_=leaving[:])
 
             for k in range(len(blocks2) + 2):
                 if k < len(blocks2):

@@ -27,7 +27,7 @@ MULTIPLY_LAG = 3
 TANH_LAG = 6
 MIX_LAG = 7
 CAST_LAG = 8
-WARM_UP = 6
+QUANTISE_LAG = 9
 
 FLOPS = 2 * (ROOTS + SIDES * ROOTS) * (SIDES * GATES * H) * H
 
@@ -116,12 +116,11 @@ def tile_decodertreernn_pa_kernel(
                 bias=bias_rz_column(side, gate, blk, e), scale=1.0,
             )
 
-        def reset_candidate(cand, bank, reset, side, blk):
-            for e in range(PAIR):
-                nc.vector.scalar_tensor_tensor(
-                    out=cand[:, e, :], in0=bank[:, e, :], scalar=bias_column(side, 1, 2, blk, e),
-                    in1=reset[:, e, :], op0=ALU.add, op1=ALU.mult,
-                )
+        def reset_candidate(cand, bank, reset, side, blk, e):
+            nc.vector.scalar_tensor_tensor(
+                out=cand[:, e, :], in0=bank[:, e, :], scalar=bias_column(side, 1, 2, blk, e),
+                in1=reset[:, e, :], op0=ALU.add, op1=ALU.mult,
+            )
 
         def tanh(cand, side, blk, e):
             nc.scalar.activation(
@@ -129,17 +128,13 @@ def tile_decodertreernn_pa_kernel(
                 bias=bias_column(side, 0, 2, blk, e), scale=1.0,
             )
 
-        def mix_begin(diff, prev, cand, update):
-            nc.vector.tensor_sub(out=diff[:], in0=prev, in1=cand[:])
-            nc.vector.tensor_mul(out=diff[:], in0=update[:], in1=diff[:])
-
         with tc.tile_pool(name="raw", bufs=SLABS) as raw_pool, tc.tile_pool(
             name="once", bufs=1
         ) as once, tc.tile_pool(name="stage", bufs=4) as stage, tc.tile_pool(
             name="work1", bufs=3
-        ) as work1, tc.psum_pool(name="flip", bufs=4) as flip_psum, tc.psum_pool(
+        ) as work1, tc.psum_pool(name="flip", bufs=5) as flip_psum, tc.psum_pool(
             name="gates1", bufs=3
-        ) as gates1, tc.psum_pool(name="idle", bufs=1) as idle_psum:
+        ) as gates1:
             x_raw = once.tile([P, H], BF16)
             nc.sync.dma_start(out=x_raw[:], in_=h_nodes.flatten_outer_dims())
             raw = []
@@ -159,29 +154,6 @@ def tile_decodertreernn_pa_kernel(
             warm = once.tile([P, 1], F32)
             nc.vector.memset(warm[:], 0.0)
             nc.scalar.activation(out=warm[:], in_=warm[:], func=ACT.Sigmoid)
-
-            zeros = once.tile([P, BANK], BF16)
-            nc.vector.memset(zeros[:], 0.0)
-            unread = idle_psum.tile([P, BANK], F32)
-
-            def idle_matmuls(count):
-                for i in range(count):
-                    nc.tensor.matmul(
-                        out=unread[:], lhsT=zeros[:, 0:P], rhs=zeros[:], start=True, stop=True
-                    )
-
-            def idle_pass(n):
-                nc.tensor.matmul_mx(
-                    out=unread[:],
-                    lhsT=x_codes[0][:].bitcast(FP8X4),
-                    lhsT_scale=x_scales[0][:],
-                    rhs=w_codes[n][:].bitcast(FP8X4),
-                    rhs_scale=w_scales[n][:],
-                    start=True,
-                    stop=True,
-                )
-
-            idle_matmuls(WARM_UP)
 
             x_words = x_raw[:].bitcast(F32)
             x_flipped = flip_psum.tile([P, BANK], F32, name="flipped")
@@ -273,27 +245,36 @@ def tile_decodertreernn_pa_kernel(
                     gate_out[i] = work1.tile([P, PAIR, ROOTS], F32, name=("reset", "update")[gate])
                 sigmoid(gate_out[i], sums[m], side, gate, blk, e)
 
-            def mix(n):
-                lag = (MIX_LAG, CAST_LAG, MULTIPLY_LAG)[n % GATES]
-                m = n - lag
-                if not 0 <= m < SLABS:
-                    return
-                blk, side, gate = slabs[m]
-                i = m // GATES
-                nodes = slice(side * ROOTS, (side + 1) * ROOTS)
-                if lag == MULTIPLY_LAG:
-                    cand[i] = work1.tile([P, PAIR, ROOTS], F32, name="cand")
-                    reset_candidate(cand[i], sums[m], reset[i], side, blk)
-                elif lag == MIX_LAG:
-                    diff[i] = work1.tile([P, PAIR, ROOTS], F32, name="diff")
-                    mix_begin(diff[i], x_f32[:, blk, :, :], cand[i], update[i])
-                else:
-                    nc.vector.tensor_add(out=c_f32[blk][:, :, nodes], in0=diff[i][:], in1=cand[i][:])
+            def vector_share(n, half):
+                turn = n % GATES
+                m = n - (MIX_LAG, CAST_LAG, MULTIPLY_LAG)[turn]
+                if 0 <= m < SLABS:
+                    blk, side, gate = slabs[m]
+                    i = m // GATES
+                    nodes = slice(side * ROOTS, (side + 1) * ROOTS)
                     g, u = divmod(blk, PAIR)
-                    nc.vector.tensor_copy(
-                        out=c_grouped[g][:, nodes, u * PAIR : (u + 1) * PAIR],
-                        in_=c_f32[blk][:, :, nodes].rearrange("p e j -> p j e"),
-                    )
+                    if turn == 2:
+                        if half == 0:
+                            cand[i] = work1.tile([P, PAIR, ROOTS], F32, name="cand")
+                        reset_candidate(cand[i], sums[m], reset[i], side, blk, half)
+                    elif turn == 0 and half == 0:
+                        diff[i] = work1.tile([P, PAIR, ROOTS], F32, name="diff")
+                        nc.vector.tensor_sub(out=diff[i][:], in0=x_f32[:, blk, :, :], in1=cand[i][:])
+                    elif turn == 0:
+                        nc.vector.tensor_mul(out=diff[i][:], in0=update[i][:], in1=diff[i][:])
+                    elif half == 0:
+                        nc.vector.tensor_add(
+                            out=c_f32[blk][:, :, nodes], in0=diff[i][:], in1=cand[i][:]
+                        )
+                    else:
+                        nc.vector.tensor_copy(
+                            out=c_grouped[g][:, nodes, u * PAIR : (u + 1) * PAIR],
+                            in_=c_f32[blk][:, :, nodes].rearrange("p e j -> p j e"),
+                        )
+                m = n - QUANTISE_LAG
+                if turn == 2 and half == 1 and 0 <= m < SLABS:
+                    blk, side, gate = slabs[m]
+                    g, u = divmod(blk, PAIR)
                     if u == PAIR - 1 and side == SIDES - 1:
                         nc.vector.quantize_mx(
                             out=c_codes[g][:].bitcast(FP8X4),
@@ -301,24 +282,21 @@ def tile_decodertreernn_pa_kernel(
                             in_=c_grouped[g][:].rearrange("p c t -> p (c t)"),
                         )
 
-            for n in range(SLABS + CAST_LAG + 1):
+            for n in range(SLABS + QUANTISE_LAG + 1):
                 if n < SLABS:
                     transpose_slab(n)
-                if n < MULTIPLY_LAG:
-                    idle_matmuls(1)
-                else:
-                    if n - MULTIPLY_LAG < SLABS:
-                        multiply_slab(n - MULTIPLY_LAG)
-                    idle_pass(min(n - MULTIPLY_LAG, SLABS - 1))
+                if 0 <= n - MULTIPLY_LAG < SLABS:
+                    multiply_slab(n - MULTIPLY_LAG)
+                vector_share(n, 0)
                 if 0 <= n - 1 < SLABS:
                     quantise_slab(n - 1)
+                vector_share(n, 1)
                 for e in range(PAIR):
                     if n < SLABS:
                         empty_bank(n, e)
                     activate(n, e)
-                mix(n)
 
-        with tc.tile_pool(name="work2", bufs=3) as work2, tc.psum_pool(
+        with tc.tile_pool(name="work2", bufs=4) as work2, tc.psum_pool(
             name="gates2", bufs=2
         ) as gates2, tc.psum_pool(name="back", bufs=2) as back_psum:
             children = SIDES * ROOTS
@@ -341,17 +319,32 @@ def tile_decodertreernn_pa_kernel(
                 cand2[k] = work2.tile([P, PAIR, children], F32, name="cand2")
                 for e in range(PAIR):
                     sigmoid(reset2, banks[0], side2, 0, blk, e)
+                if k >= 1:
+                    mix_begin(k - 1)
+                for e in range(PAIR):
+                    reset_candidate(cand2[k], banks[2], reset2, side2, blk, e)
                 for e in range(PAIR):
                     sigmoid(update2[k], banks[1], side2, 1, blk, e)
-                reset_candidate(cand2[k], banks[2], reset2, side2, blk)
                 for e in range(PAIR):
                     tanh(cand2[k], side2, blk, e)
 
-            def mix_block(k):
+            def mix_begin(k):
                 side2, blk = blocks2[k]
                 mixed[k] = work2.tile([P, PAIR, children], F32, name="mixed")
-                mix_begin(mixed[k], c_f32[blk][:], cand2[k], update2[k])
-                nc.vector.tensor_add(out=mixed[k][:], in0=mixed[k][:], in1=cand2[k][:])
+                for e in range(PAIR):
+                    nc.vector.tensor_sub(
+                        out=mixed[k][:, e, :], in0=c_f32[blk][:, e, :], in1=cand2[k][:, e, :]
+                    )
+
+            def mix_end(k):
+                for e in range(PAIR):
+                    nc.vector.tensor_mul(
+                        out=mixed[k][:, e, :], in0=update2[k][:, e, :], in1=mixed[k][:, e, :]
+                    )
+                for e in range(PAIR):
+                    nc.vector.tensor_add(
+                        out=mixed[k][:, e, :], in0=mixed[k][:, e, :], in1=cand2[k][:, e, :]
+                    )
 
             def transpose_back(k):
                 back[k] = back_psum.tile([P, SIDES, PAIR, P], F32, name="back")
@@ -371,14 +364,17 @@ def tile_decodertreernn_pa_kernel(
                 )
                 nc.sync.dma_start(out=out_rows[:, :, side2, cols], in_=leaving[:])
 
-            for k in range(len(blocks2) + 2):
-                if k < len(blocks2):
+            count = len(blocks2)
+            for k in range(count + 3):
+                if k < count:
                     banks = gates_of_block(k)
-                if k >= 2:
-                    transpose_back(k - 2)
-                if k < len(blocks2):
+                if k >= 3:
+                    transpose_back(k - 3)
+                if k < count:
                     activate_block(k, banks)
-                if k >= 2:
-                    store_block(k - 2)
-                if 1 <= k <= len(blocks2):
-                    mix_block(k - 1)
+                elif k == count:
+                    mix_begin(k - 1)
+                if 1 <= k <= count:
+                    mix_end(k - 1)
+                if k >= 3:
+                    store_block(k - 3)

@@ -15,19 +15,13 @@ GATES = 3
 SIDES = 2
 PAIR = 2
 ROOTS = 128
+CHILDREN = SIDES * ROOTS
 BLOCK = P * PAIR
 BLOCKS = H // BLOCK
 PASSES = H // (4 * P)
 WORD_BLOCKS = H // BLOCK
 BANK = 512
-SLABS = SIDES * BLOCKS * GATES
 SLAB_WORDS = PAIR * PASSES * P
-
-MULTIPLY_LAG = 3
-TANH_LAG = 6
-MIX_LAG = 7
-CAST_LAG = 8
-QUANTISE_LAG = 9
 
 FLOPS = 2 * (ROOTS + SIDES * ROOTS) * (SIDES * GATES * H) * H
 
@@ -42,49 +36,35 @@ def tile_decodertreernn_pa_kernel(
         for w in (Whh_l, Whh_r)
     ]
     out_rows = out.rearrange("b (i s s2) h -> (b i) s s2 h", s=SIDES, s2=SIDES)
+    blocks = [(side, blk) for blk in range(BLOCKS) for side in range(SIDES)]
 
-    slabs = [
-        (blk, side, gate)
-        for blk in range(BLOCKS)
-        for side in range(SIDES)
-        for gate in range(GATES)
-    ]
-
-    def slab_index(blk, side, gate):
-        return (blk * SIDES + side) * GATES + gate
-
-    with tc.manual_schedule(), tc.tile_pool(name="keep", bufs=1) as keep:
+    with tc.tile_pool(name="keep", bufs=1) as keep:
         identity = keep.tile([P, P], F32)
         make_identity(nc, identity[:])
 
-        w_codes = [
-            keep.tile([P, SLAB_WORDS], U32, align_bytes=64, name="w_codes%d" % n) for n in range(SLABS)
-        ]
-        w_scales = [
-            keep.tile([P, SLAB_WORDS], U8, align_bytes=64, name="w_scales%d" % n) for n in range(SLABS)
-        ]
-        x_codes = [
-            keep.tile([P, ROOTS], U32, align_bytes=64, name="x_codes%d" % g) for g in range(PASSES)
-        ]
-        x_scales = [
-            keep.tile([P, ROOTS], U8, align_bytes=64, name="x_scales%d" % g) for g in range(PASSES)
-        ]
-        c_codes = [
-            keep.tile([P, SIDES * ROOTS], U32, align_bytes=64, name="c_codes%d" % g)
-            for g in range(PASSES)
-        ]
-        c_scales = [
-            keep.tile([P, SIDES * ROOTS], U8, align_bytes=64, name="c_scales%d" % g)
-            for g in range(PASSES)
-        ]
+        w_codes, w_scales = {}, {}
+        for side, blk in blocks:
+            for gate in range(GATES):
+                slab = (side, blk, gate)
+                w_codes[slab] = keep.tile(
+                    [P, SLAB_WORDS], U32, align_bytes=64, name="w_codes%d%d%d" % slab
+                )
+                w_scales[slab] = keep.tile(
+                    [P, SLAB_WORDS], U8, align_bytes=64, name="w_scales%d%d%d" % slab
+                )
+        x_codes, x_scales, c_codes, c_scales, c_grouped = [], [], [], [], []
+        for g in range(PASSES):
+            x_codes.append(keep.tile([P, ROOTS], U32, align_bytes=64, name="x_codes%d" % g))
+            x_scales.append(keep.tile([P, ROOTS], U8, align_bytes=64, name="x_scales%d" % g))
+            c_codes.append(keep.tile([P, CHILDREN], U32, align_bytes=64, name="c_codes%d" % g))
+            c_scales.append(keep.tile([P, CHILDREN], U8, align_bytes=64, name="c_scales%d" % g))
+            c_grouped.append(
+                keep.tile([P, CHILDREN, 2 * PAIR], BF16, align_bytes=64, name="c_grouped%d" % g)
+            )
         x_f32 = keep.tile([P, BLOCKS, PAIR, ROOTS], F32)
-        c_f32 = [
-            keep.tile([P, PAIR, SIDES * ROOTS], F32, name="c_f32_%d" % blk) for blk in range(BLOCKS)
-        ]
-        c_grouped = [
-            keep.tile([P, SIDES * ROOTS, 2 * PAIR], BF16, align_bytes=64, name="c_grouped%d" % g)
-            for g in range(PASSES)
-        ]
+        c_f32 = {}
+        for side, blk in blocks:
+            c_f32[(side, blk)] = keep.tile([P, PAIR, ROOTS], F32, name="c_f32_%d%d" % (side, blk))
         bias = keep.tile([P, SIDES * 2 * GATES * BLOCKS * PAIR], F32)
         bias_rz = keep.tile([P, SIDES, 2 * BLOCKS * PAIR], F32)
 
@@ -96,52 +76,71 @@ def tile_decodertreernn_pa_kernel(
             col = (gate * BLOCKS + blk) * PAIR + e
             return bias_rz[:, side, col : col + 1]
 
-        def multiply(bank, slab, codes, scales):
+        def gru_round(side, blk, codes, scales, prev, sums_psum, work):
+            width = len(prev) * ROOTS
+            sums = []
+            for gate in range(GATES):
+                gate_sums = sums_psum.tile([P, PAIR, width], F32, name="gate_sums")
+                slab = (side, blk, gate)
+                for e in range(PAIR):
+                    for g in range(PASSES):
+                        first = (e * PASSES + g) * P
+                        nc.tensor.matmul_mx(
+                            out=gate_sums[:, e, :],
+                            lhsT=w_codes[slab][:, first : first + P].bitcast(FP8X4),
+                            lhsT_scale=w_scales[slab][:, first : first + P],
+                            rhs=codes[g][:].bitcast(FP8X4),
+                            rhs_scale=scales[g][:],
+                            start=(g == 0),
+                            stop=(g == PASSES - 1),
+                        )
+                sums.append(gate_sums)
+
+            reset = work.tile([P, PAIR, width], F32)
+            update = work.tile([P, PAIR, width], F32)
+            cand = work.tile([P, PAIR, width], F32)
             for e in range(PAIR):
-                for g in range(PASSES):
-                    first = (e * PASSES + g) * P
-                    nc.tensor.matmul_mx(
-                        out=bank[:, e, :],
-                        lhsT=w_codes[slab][:, first : first + P].bitcast(FP8X4),
-                        lhsT_scale=w_scales[slab][:, first : first + P],
-                        rhs=codes[g][:].bitcast(FP8X4),
-                        rhs_scale=scales[g][:],
-                        start=(g == 0),
-                        stop=(g == PASSES - 1),
-                    )
+                nc.scalar.activation(
+                    out=reset[:, e, :], in_=sums[0][:, e, :], func=ACT.Sigmoid,
+                    bias=bias_rz_column(side, 0, blk, e), scale=1.0,
+                )
+            for e in range(PAIR):
+                nc.scalar.activation(
+                    out=update[:, e, :], in_=sums[1][:, e, :], func=ACT.Sigmoid,
+                    bias=bias_rz_column(side, 1, blk, e), scale=1.0,
+                )
+            for e in range(PAIR):
+                nc.vector.scalar_tensor_tensor(
+                    out=cand[:, e, :], in0=sums[2][:, e, :], scalar=bias_column(side, 1, 2, blk, e),
+                    in1=reset[:, e, :], op0=ALU.add, op1=ALU.mult,
+                )
+            for e in range(PAIR):
+                nc.scalar.activation(
+                    out=cand[:, e, :], in_=cand[:, e, :], func=ACT.Tanh,
+                    bias=bias_column(side, 0, 2, blk, e), scale=1.0,
+                )
+            parts = [slice(i * ROOTS, (i + 1) * ROOTS) for i in range(len(prev))]
+            diffs = [work.tile([P, PAIR, ROOTS], F32, name="diff") for part in parts]
+            for x, part, diff in zip(prev, parts, diffs):
+                nc.vector.tensor_sub(out=diff[:], in0=x, in1=cand[:, :, part])
+            for part, diff in zip(parts, diffs):
+                nc.vector.tensor_mul(out=diff[:], in0=update[:, :, part], in1=diff[:])
+            return [(diff, cand[:, :, part]) for part, diff in zip(parts, diffs)]
 
-        def sigmoid(gate_out, bank, side, gate, blk, e):
-            nc.scalar.activation(
-                out=gate_out[:, e, :], in_=bank[:, e, :], func=ACT.Sigmoid,
-                bias=bias_rz_column(side, gate, blk, e), scale=1.0,
-            )
-
-        def reset_candidate(cand, bank, reset, side, blk, e):
-            nc.vector.scalar_tensor_tensor(
-                out=cand[:, e, :], in0=bank[:, e, :], scalar=bias_column(side, 1, 2, blk, e),
-                in1=reset[:, e, :], op0=ALU.add, op1=ALU.mult,
-            )
-
-        def tanh(cand, side, blk, e):
-            nc.scalar.activation(
-                out=cand[:, e, :], in_=cand[:, e, :], func=ACT.Tanh,
-                bias=bias_column(side, 0, 2, blk, e), scale=1.0,
-            )
-
-        with tc.tile_pool(name="raw", bufs=SLABS) as raw_pool, tc.tile_pool(
+        with tc.tile_pool(name="raw", bufs=len(blocks) * GATES) as raw_pool, tc.tile_pool(
             name="once", bufs=1
         ) as once, tc.tile_pool(name="stage", bufs=4) as stage, tc.tile_pool(
             name="work1", bufs=3
         ) as work1, tc.psum_pool(name="flip", bufs=5) as flip_psum, tc.psum_pool(
-            name="gates1", bufs=3
-        ) as gates1:
+            name="sums1", bufs=3
+        ) as sums1:
             x_raw = once.tile([P, H], BF16)
             nc.sync.dma_start(out=x_raw[:], in_=h_nodes.flatten_outer_dims())
-            raw = []
-            for blk, side, gate in slabs:
-                raw_slab = raw_pool.tile([P, PAIR * H], BF16, name="raw_slab")
-                nc.sync.dma_start(out=raw_slab[:], in_=slab_rows[side][gate, blk])
-                raw.append(raw_slab)
+            raw = {}
+            for side, blk in blocks:
+                for gate in range(GATES):
+                    raw[(side, blk, gate)] = raw_pool.tile([P, PAIR * H], BF16, name="raw_slab")
+                    nc.sync.dma_start(out=raw[(side, blk, gate)][:], in_=slab_rows[side][gate, blk])
             bias_raw = once.tile([P, BLOCK], BF16)
             nc.vector.memset(bias_raw[:], 0.0)
             for v, vec in enumerate((bih_l, bhh_l, bih_r, bhh_r)):
@@ -172,6 +171,12 @@ def tile_decodertreernn_pa_kernel(
                     "p (blk j e) -> p blk e j", blk=BLOCKS, e=PAIR
                 ),
             )
+            for g in range(PASSES):
+                nc.vector.quantize_mx(
+                    out=x_codes[g][:].bitcast(FP8X4),
+                    scales=x_scales[g][:],
+                    in_=x_grouped[:, g * BLOCK : (g + 1) * BLOCK].bitcast(BF16),
+                )
 
             b_flipped = flip_psum.tile([P, BANK], F32, name="flipped")
             nc.tensor.transpose(b_flipped[:, 0:P], bias_raw[:].bitcast(F32), identity[:])
@@ -182,199 +187,71 @@ def tile_decodertreernn_pa_kernel(
             nc.vector.tensor_add(
                 out=bias_rz[:], in0=by_kind[:, :, 0, 0:rz_cols], in1=by_kind[:, :, 1, 0:rz_cols]
             )
-            for g in range(PASSES):
-                nc.vector.quantize_mx(
-                    out=x_codes[g][:].bitcast(FP8X4),
-                    scales=x_scales[g][:],
-                    in_=x_grouped[:, g * BLOCK : (g + 1) * BLOCK].bitcast(BF16),
-                )
 
-            flipped = {}
-            grouped = {}
-            sums = {}
-            reset, update, cand, diff = {}, {}, {}, {}
-
-            def transpose_slab(n):
-                words = raw[n][:].bitcast(F32)
+            def quantise_slab(slab):
+                words = raw[slab][:].bitcast(F32)
+                grouped = stage.tile([P, PAIR * BANK], F32, align_bytes=64)
                 for e in range(PAIR):
-                    flipped[(n, e)] = flip_psum.tile([P, BANK], F32, name="flipped")
+                    flipped = flip_psum.tile([P, BANK], F32)
                     for w in range(WORD_BLOCKS):
                         first = (e * WORD_BLOCKS + w) * P
                         nc.tensor.transpose(
-                            flipped[(n, e)][:, w * P : (w + 1) * P],
-                            words[:, first : first + P],
-                            identity[:],
+                            flipped[:, w * P : (w + 1) * P], words[:, first : first + P], identity[:]
                         )
-
-            def empty_bank(n, e):
-                if e == 0:
-                    grouped[n] = stage.tile([P, PAIR * BANK], F32, align_bytes=64, name="grouped")
-                by_vector = n % GATES == GATES - 1 and e == PAIR - 1
-                copy = nc.vector.tensor_copy if by_vector else nc.scalar.copy
-                copy(
-                    out=grouped[n][:, e * BANK : (e + 1) * BANK].rearrange(
-                        "p (g q u) -> p g q u", g=PASSES, u=PAIR
-                    ),
-                    in_=flipped[(n, e)][:].rearrange("p (g u q) -> p g q u", g=PASSES, u=PAIR),
-                )
-
-            def quantise_slab(n):
+                    by_vector = slab[2] == GATES - 1 and e == PAIR - 1
+                    copy = nc.vector.tensor_copy if by_vector else nc.scalar.copy
+                    copy(
+                        out=grouped[:, e * BANK : (e + 1) * BANK].rearrange(
+                            "p (g q u) -> p g q u", g=PASSES, u=PAIR
+                        ),
+                        in_=flipped[:].rearrange("p (g u q) -> p g q u", g=PASSES, u=PAIR),
+                    )
                 nc.vector.quantize_mx(
-                    out=w_codes[n][:].bitcast(FP8X4),
-                    scales=w_scales[n][:],
-                    in_=grouped[n][:].bitcast(BF16),
+                    out=w_codes[slab][:].bitcast(FP8X4),
+                    scales=w_scales[slab][:],
+                    in_=grouped[:].bitcast(BF16),
                 )
 
-            def multiply_slab(n):
-                sums[n] = gates1.tile([P, PAIR, ROOTS], F32, name="sums")
-                multiply(sums[n], n, x_codes, x_scales)
+            def first_level(side, blk):
+                rounds = gru_round(side, blk, x_codes, x_scales, [x_f32[:, blk, :, :]], sums1, work1)
+                diff, cand = rounds[0]
+                nc.vector.tensor_add(out=c_f32[(side, blk)][:], in0=diff[:], in1=cand)
+                g, u = divmod(blk, PAIR)
+                nc.vector.tensor_copy(
+                    out=c_grouped[g][:, side * ROOTS : (side + 1) * ROOTS, u * PAIR : (u + 1) * PAIR],
+                    in_=c_f32[(side, blk)][:].rearrange("p e j -> p j e"),
+                )
+                if u == PAIR - 1 and side == SIDES - 1:
+                    nc.vector.quantize_mx(
+                        out=c_codes[g][:].bitcast(FP8X4),
+                        scales=c_scales[g][:],
+                        in_=c_grouped[g][:].rearrange("p c t -> p (c t)"),
+                    )
 
-            def activate(n, e):
-                m = n - MULTIPLY_LAG
-                if n % GATES == GATES - 1:
-                    m = n - TANH_LAG
-                if not 0 <= m < SLABS:
-                    return
-                blk, side, gate = slabs[m]
-                i = m // GATES
-                if gate == GATES - 1:
-                    tanh(cand[i], side, blk, e)
-                    return
-                gate_out = (reset, update)[gate]
-                if e == 0:
-                    gate_out[i] = work1.tile([P, PAIR, ROOTS], F32, name=("reset", "update")[gate])
-                sigmoid(gate_out[i], sums[m], side, gate, blk, e)
-
-            def vector_share(n, half):
-                turn = n % GATES
-                m = n - (MIX_LAG, CAST_LAG, MULTIPLY_LAG)[turn]
-                if 0 <= m < SLABS:
-                    blk, side, gate = slabs[m]
-                    i = m // GATES
-                    nodes = slice(side * ROOTS, (side + 1) * ROOTS)
-                    g, u = divmod(blk, PAIR)
-                    if turn == 2:
-                        if half == 0:
-                            cand[i] = work1.tile([P, PAIR, ROOTS], F32, name="cand")
-                        reset_candidate(cand[i], sums[m], reset[i], side, blk, half)
-                    elif turn == 0 and half == 0:
-                        diff[i] = work1.tile([P, PAIR, ROOTS], F32, name="diff")
-                        nc.vector.tensor_sub(out=diff[i][:], in0=x_f32[:, blk, :, :], in1=cand[i][:])
-                    elif turn == 0:
-                        nc.vector.tensor_mul(out=diff[i][:], in0=update[i][:], in1=diff[i][:])
-                    elif half == 0:
-                        nc.vector.tensor_add(
-                            out=c_f32[blk][:, :, nodes], in0=diff[i][:], in1=cand[i][:]
-                        )
-                    else:
-                        nc.vector.tensor_copy(
-                            out=c_grouped[g][:, nodes, u * PAIR : (u + 1) * PAIR],
-                            in_=c_f32[blk][:, :, nodes].rearrange("p e j -> p j e"),
-                        )
-                m = n - QUANTISE_LAG
-                if turn == 2 and half == 1 and 0 <= m < SLABS:
-                    blk, side, gate = slabs[m]
-                    g, u = divmod(blk, PAIR)
-                    if u == PAIR - 1 and side == SIDES - 1:
-                        nc.vector.quantize_mx(
-                            out=c_codes[g][:].bitcast(FP8X4),
-                            scales=c_scales[g][:],
-                            in_=c_grouped[g][:].rearrange("p c t -> p (c t)"),
-                        )
-
-            for n in range(SLABS + QUANTISE_LAG + 1):
-                if n < SLABS:
-                    transpose_slab(n)
-                if 0 <= n - MULTIPLY_LAG < SLABS:
-                    multiply_slab(n - MULTIPLY_LAG)
-                vector_share(n, 0)
-                if 0 <= n - 1 < SLABS:
-                    quantise_slab(n - 1)
-                vector_share(n, 1)
-                for e in range(PAIR):
-                    if n < SLABS:
-                        empty_bank(n, e)
-                    activate(n, e)
+            for i, (side, blk) in enumerate(blocks):
+                for gate in range(GATES):
+                    quantise_slab((side, blk, gate))
+                if i > 0:
+                    first_level(*blocks[i - 1])
+            first_level(*blocks[-1])
 
         with tc.tile_pool(name="work2", bufs=4) as work2, tc.psum_pool(
-            name="gates2", bufs=2
-        ) as gates2, tc.psum_pool(name="back", bufs=2) as back_psum:
-            children = SIDES * ROOTS
-            blocks2 = [(side2, blk) for side2 in range(SIDES) for blk in range(BLOCKS)]
-            update2, cand2, mixed, back = {}, {}, {}, {}
-
-            def gates_of_block(k):
-                side2, blk = blocks2[k]
-                banks = []
-                for gate in range(GATES):
-                    bank = gates2.tile([P, PAIR, children], F32, name="sums%d" % gate)
-                    multiply(bank, slab_index(blk, side2, gate), c_codes, c_scales)
-                    banks.append(bank)
-                return banks
-
-            def activate_block(k, banks):
-                side2, blk = blocks2[k]
-                reset2 = work2.tile([P, PAIR, children], F32)
-                update2[k] = work2.tile([P, PAIR, children], F32, name="update2")
-                cand2[k] = work2.tile([P, PAIR, children], F32, name="cand2")
-                for e in range(PAIR):
-                    sigmoid(reset2, banks[0], side2, 0, blk, e)
-                if k >= 1:
-                    mix_begin(k - 1)
-                for e in range(PAIR):
-                    reset_candidate(cand2[k], banks[2], reset2, side2, blk, e)
-                for e in range(PAIR):
-                    sigmoid(update2[k], banks[1], side2, 1, blk, e)
-                for e in range(PAIR):
-                    tanh(cand2[k], side2, blk, e)
-
-            def mix_begin(k):
-                side2, blk = blocks2[k]
-                mixed[k] = work2.tile([P, PAIR, children], F32, name="mixed")
-                for e in range(PAIR):
-                    nc.vector.tensor_sub(
-                        out=mixed[k][:, e, :], in0=c_f32[blk][:, e, :], in1=cand2[k][:, e, :]
-                    )
-
-            def mix_end(k):
-                for e in range(PAIR):
-                    nc.vector.tensor_mul(
-                        out=mixed[k][:, e, :], in0=update2[k][:, e, :], in1=mixed[k][:, e, :]
-                    )
-                for e in range(PAIR):
-                    nc.vector.tensor_add(
-                        out=mixed[k][:, e, :], in0=mixed[k][:, e, :], in1=cand2[k][:, e, :]
-                    )
-
-            def transpose_back(k):
-                back[k] = back_psum.tile([P, SIDES, PAIR, P], F32, name="back")
-                for s in range(SIDES):
+            name="sums2", bufs=6
+        ) as sums2, tc.psum_pool(name="back", bufs=2) as back_psum:
+            for side2, blk in blocks:
+                rounds = gru_round(
+                    side2, blk, c_codes, c_scales, [c_f32[(s, blk)][:] for s in range(SIDES)],
+                    sums2, work2,
+                )
+                back = back_psum.tile([P, SIDES, PAIR, P], F32)
+                for s, (diff, cand) in enumerate(rounds):
+                    nc.vector.tensor_add(out=diff[:], in0=diff[:], in1=cand)
                     for e in range(PAIR):
-                        nc.tensor.transpose(
-                            back[k][:, s, e, :], mixed[k][:, e, s * ROOTS : (s + 1) * ROOTS], identity[:]
-                        )
-
-            def store_block(k):
-                side2, blk = blocks2[k]
-                cols = slice(blk * BLOCK, (blk + 1) * BLOCK)
+                        nc.tensor.transpose(back[:, s, e, :], diff[:, e, :], identity[:])
                 leaving = work2.tile([P, SIDES, BLOCK], F32)
                 nc.scalar.copy(
                     out=leaving[:].rearrange("j s (q e) -> j s q e", e=PAIR),
-                    in_=back[k][:].rearrange("j s e q -> j s q e"),
+                    in_=back[:].rearrange("j s e q -> j s q e"),
                 )
+                cols = slice(blk * BLOCK, (blk + 1) * BLOCK)
                 nc.sync.dma_start(out=out_rows[:, :, side2, cols], in_=leaving[:])
-
-            count = len(blocks2)
-            for k in range(count + 3):
-                if k < count:
-                    banks = gates_of_block(k)
-                if k >= 3:
-                    transpose_back(k - 3)
-                if k < count:
-                    activate_block(k, banks)
-                elif k == count:
-                    mix_begin(k - 1)
-                if 1 <= k <= count:
-                    mix_end(k - 1)
-                if k >= 3:
-                    store_block(k - 3)

@@ -12,16 +12,24 @@ ALU = mybir.AluOpType
 P = 128
 H = 1024
 GATES = 3
+RESET, UPDATE, CANDIDATE = 0, 1, 2
+LOAD_ORDER = [RESET, CANDIDATE, UPDATE]
 SIDES = 2
 PAIR = 2
 ROOTS = 128
-CHILDREN = SIDES * ROOTS
 BLOCK = P * PAIR
 BLOCKS = H // BLOCK
 PASSES = H // (4 * P)
 WORD_BLOCKS = H // BLOCK
 BANK = 512
+SLABS = SIDES * BLOCKS * GATES
 SLAB_WORDS = PAIR * PASSES * P
+
+MULTIPLY_LAG = 3
+TANH_LAG = 6
+MIX_LAG = 7
+SUM_LAG = 8
+RUN = 2
 
 FLOPS = 2 * (ROOTS + SIDES * ROOTS) * (SIDES * GATES * H) * H
 
@@ -36,35 +44,49 @@ def tile_decodertreernn_pa_kernel(
         for w in (Whh_l, Whh_r)
     ]
     out_rows = out.rearrange("b (i s s2) h -> (b i) s s2 h", s=SIDES, s2=SIDES)
-    blocks = [(side, blk) for blk in range(BLOCKS) for side in range(SIDES)]
 
-    with tc.tile_pool(name="keep", bufs=1) as keep:
+    slabs = [
+        (blk, side, gate)
+        for blk in range(BLOCKS)
+        for side in range(SIDES)
+        for gate in LOAD_ORDER
+    ]
+
+    def slab_index(blk, side, gate):
+        return (blk * SIDES + side) * GATES + LOAD_ORDER.index(gate)
+
+    with tc.manual_schedule(), tc.tile_pool(name="keep", bufs=1) as keep:
         identity = keep.tile([P, P], F32)
         make_identity(nc, identity[:])
 
-        w_codes, w_scales = {}, {}
-        for side, blk in blocks:
-            for gate in range(GATES):
-                slab = (side, blk, gate)
-                w_codes[slab] = keep.tile(
-                    [P, SLAB_WORDS], U32, align_bytes=64, name="w_codes%d%d%d" % slab
-                )
-                w_scales[slab] = keep.tile(
-                    [P, SLAB_WORDS], U8, align_bytes=64, name="w_scales%d%d%d" % slab
-                )
-        x_codes, x_scales, c_codes, c_scales, c_grouped = [], [], [], [], []
-        for g in range(PASSES):
-            x_codes.append(keep.tile([P, ROOTS], U32, align_bytes=64, name="x_codes%d" % g))
-            x_scales.append(keep.tile([P, ROOTS], U8, align_bytes=64, name="x_scales%d" % g))
-            c_codes.append(keep.tile([P, CHILDREN], U32, align_bytes=64, name="c_codes%d" % g))
-            c_scales.append(keep.tile([P, CHILDREN], U8, align_bytes=64, name="c_scales%d" % g))
-            c_grouped.append(
-                keep.tile([P, CHILDREN, 2 * PAIR], BF16, align_bytes=64, name="c_grouped%d" % g)
-            )
+        w_codes = [
+            keep.tile([P, SLAB_WORDS], U32, align_bytes=64, name="w_codes%d" % n) for n in range(SLABS)
+        ]
+        w_scales = [
+            keep.tile([P, SLAB_WORDS], U8, align_bytes=64, name="w_scales%d" % n) for n in range(SLABS)
+        ]
+        x_codes = [
+            keep.tile([P, ROOTS], U32, align_bytes=64, name="x_codes%d" % g) for g in range(PASSES)
+        ]
+        x_scales = [
+            keep.tile([P, ROOTS], U8, align_bytes=64, name="x_scales%d" % g) for g in range(PASSES)
+        ]
+        c_codes = [
+            keep.tile([P, SIDES * ROOTS], U32, align_bytes=64, name="c_codes%d" % g)
+            for g in range(PASSES)
+        ]
+        c_scales = [
+            keep.tile([P, SIDES * ROOTS], U8, align_bytes=64, name="c_scales%d" % g)
+            for g in range(PASSES)
+        ]
         x_f32 = keep.tile([P, BLOCKS, PAIR, ROOTS], F32)
-        c_f32 = {}
-        for side, blk in blocks:
-            c_f32[(side, blk)] = keep.tile([P, PAIR, ROOTS], F32, name="c_f32_%d%d" % (side, blk))
+        c_f32 = [
+            keep.tile([P, PAIR, SIDES * ROOTS], F32, name="c_f32_%d" % blk) for blk in range(BLOCKS)
+        ]
+        c_grouped = [
+            keep.tile([P, SIDES * ROOTS, 2 * PAIR], BF16, align_bytes=64, name="c_grouped%d" % g)
+            for g in range(PASSES)
+        ]
         bias = keep.tile([P, SIDES * 2 * GATES * BLOCKS * PAIR], F32)
         bias_rz = keep.tile([P, SIDES, 2 * BLOCKS * PAIR], F32)
 
@@ -76,71 +98,52 @@ def tile_decodertreernn_pa_kernel(
             col = (gate * BLOCKS + blk) * PAIR + e
             return bias_rz[:, side, col : col + 1]
 
-        def gru_round(side, blk, codes, scales, prev, sums_psum, work):
-            width = len(prev) * ROOTS
-            sums = []
-            for gate in range(GATES):
-                gate_sums = sums_psum.tile([P, PAIR, width], F32, name="gate_sums")
-                slab = (side, blk, gate)
-                for e in range(PAIR):
-                    for g in range(PASSES):
-                        first = (e * PASSES + g) * P
-                        nc.tensor.matmul_mx(
-                            out=gate_sums[:, e, :],
-                            lhsT=w_codes[slab][:, first : first + P].bitcast(FP8X4),
-                            lhsT_scale=w_scales[slab][:, first : first + P],
-                            rhs=codes[g][:].bitcast(FP8X4),
-                            rhs_scale=scales[g][:],
-                            start=(g == 0),
-                            stop=(g == PASSES - 1),
-                        )
-                sums.append(gate_sums)
+        def multiply(bank, slab, codes, scales):
+            for e in range(PAIR):
+                for g in range(PASSES):
+                    first = (e * PASSES + g) * P
+                    nc.tensor.matmul_mx(
+                        out=bank[:, e, :],
+                        lhsT=w_codes[slab][:, first : first + P].bitcast(FP8X4),
+                        lhsT_scale=w_scales[slab][:, first : first + P],
+                        rhs=codes[g][:].bitcast(FP8X4),
+                        rhs_scale=scales[g][:],
+                        start=(g == 0),
+                        stop=(g == PASSES - 1),
+                    )
 
-            reset = work.tile([P, PAIR, width], F32)
-            update = work.tile([P, PAIR, width], F32)
-            cand = work.tile([P, PAIR, width], F32)
-            for e in range(PAIR):
-                nc.scalar.activation(
-                    out=reset[:, e, :], in_=sums[0][:, e, :], func=ACT.Sigmoid,
-                    bias=bias_rz_column(side, 0, blk, e), scale=1.0,
-                )
-            for e in range(PAIR):
-                nc.scalar.activation(
-                    out=update[:, e, :], in_=sums[1][:, e, :], func=ACT.Sigmoid,
-                    bias=bias_rz_column(side, 1, blk, e), scale=1.0,
-                )
-            for e in range(PAIR):
-                nc.vector.scalar_tensor_tensor(
-                    out=cand[:, e, :], in0=sums[2][:, e, :], scalar=bias_column(side, 1, 2, blk, e),
-                    in1=reset[:, e, :], op0=ALU.add, op1=ALU.mult,
-                )
-            for e in range(PAIR):
-                nc.scalar.activation(
-                    out=cand[:, e, :], in_=cand[:, e, :], func=ACT.Tanh,
-                    bias=bias_column(side, 0, 2, blk, e), scale=1.0,
-                )
-            parts = [slice(i * ROOTS, (i + 1) * ROOTS) for i in range(len(prev))]
-            diffs = [work.tile([P, PAIR, ROOTS], F32, name="diff") for part in parts]
-            for x, part, diff in zip(prev, parts, diffs):
-                nc.vector.tensor_sub(out=diff[:], in0=x, in1=cand[:, :, part])
-            for part, diff in zip(parts, diffs):
-                nc.vector.tensor_mul(out=diff[:], in0=update[:, :, part], in1=diff[:])
-            return [(diff, cand[:, :, part]) for part, diff in zip(parts, diffs)]
+        def sigmoid(gate_out, bank, side, gate, blk, e):
+            nc.scalar.activation(
+                out=gate_out[:, e, :], in_=bank[:, e, :], func=ACT.Sigmoid,
+                bias=bias_rz_column(side, gate, blk, e), scale=1.0,
+            )
 
-        with tc.tile_pool(name="raw", bufs=len(blocks) * GATES) as raw_pool, tc.tile_pool(
+        def reset_candidate(cand, bank, reset, side, blk, e):
+            nc.vector.scalar_tensor_tensor(
+                out=cand[:, e, :], in0=bank[:, e, :], scalar=bias_column(side, 1, CANDIDATE, blk, e),
+                in1=reset[:, e, :], op0=ALU.add, op1=ALU.mult,
+            )
+
+        def tanh(cand, side, blk, e):
+            nc.scalar.activation(
+                out=cand[:, e, :], in_=cand[:, e, :], func=ACT.Tanh,
+                bias=bias_column(side, 0, CANDIDATE, blk, e), scale=1.0,
+            )
+
+        with tc.tile_pool(name="raw", bufs=SLABS) as raw_pool, tc.tile_pool(
             name="once", bufs=1
         ) as once, tc.tile_pool(name="stage", bufs=4) as stage, tc.tile_pool(
             name="work1", bufs=3
         ) as work1, tc.psum_pool(name="flip", bufs=5) as flip_psum, tc.psum_pool(
-            name="sums1", bufs=3
-        ) as sums1:
+            name="gates1", bufs=3
+        ) as gates1:
             x_raw = once.tile([P, H], BF16)
             nc.sync.dma_start(out=x_raw[:], in_=h_nodes.flatten_outer_dims())
-            raw = {}
-            for side, blk in blocks:
-                for gate in range(GATES):
-                    raw[(side, blk, gate)] = raw_pool.tile([P, PAIR * H], BF16, name="raw_slab")
-                    nc.sync.dma_start(out=raw[(side, blk, gate)][:], in_=slab_rows[side][gate, blk])
+            raw = []
+            for blk, side, gate in slabs:
+                raw_slab = raw_pool.tile([P, PAIR * H], BF16, name="raw_slab")
+                nc.sync.dma_start(out=raw_slab[:], in_=slab_rows[side][gate, blk])
+                raw.append(raw_slab)
             bias_raw = once.tile([P, BLOCK], BF16)
             nc.vector.memset(bias_raw[:], 0.0)
             for v, vec in enumerate((bih_l, bhh_l, bih_r, bhh_r)):
@@ -171,12 +174,6 @@ def tile_decodertreernn_pa_kernel(
                     "p (blk j e) -> p blk e j", blk=BLOCKS, e=PAIR
                 ),
             )
-            for g in range(PASSES):
-                nc.vector.quantize_mx(
-                    out=x_codes[g][:].bitcast(FP8X4),
-                    scales=x_scales[g][:],
-                    in_=x_grouped[:, g * BLOCK : (g + 1) * BLOCK].bitcast(BF16),
-                )
 
             b_flipped = flip_psum.tile([P, BANK], F32, name="flipped")
             nc.tensor.transpose(b_flipped[:, 0:P], bias_raw[:].bitcast(F32), identity[:])
@@ -187,71 +184,206 @@ def tile_decodertreernn_pa_kernel(
             nc.vector.tensor_add(
                 out=bias_rz[:], in0=by_kind[:, :, 0, 0:rz_cols], in1=by_kind[:, :, 1, 0:rz_cols]
             )
+            for g in range(PASSES):
+                nc.vector.quantize_mx(
+                    out=x_codes[g][:].bitcast(FP8X4),
+                    scales=x_scales[g][:],
+                    in_=x_grouped[:, g * BLOCK : (g + 1) * BLOCK].bitcast(BF16),
+                )
 
-            def quantise_slab(slab):
-                words = raw[slab][:].bitcast(F32)
-                grouped = stage.tile([P, PAIR * BANK], F32, align_bytes=64)
+            flipped = {}
+            grouped = {}
+            sums = {}
+            reset, update, cand, diff = {}, {}, {}, {}
+
+            def transpose_slab(n):
+                words = raw[n][:].bitcast(F32)
                 for e in range(PAIR):
-                    flipped = flip_psum.tile([P, BANK], F32)
+                    flipped[(n, e)] = flip_psum.tile([P, BANK], F32, name="flipped")
                     for w in range(WORD_BLOCKS):
                         first = (e * WORD_BLOCKS + w) * P
                         nc.tensor.transpose(
-                            flipped[:, w * P : (w + 1) * P], words[:, first : first + P], identity[:]
+                            flipped[(n, e)][:, w * P : (w + 1) * P],
+                            words[:, first : first + P],
+                            identity[:],
                         )
-                    by_vector = slab[2] == GATES - 1 and e == PAIR - 1
-                    copy = nc.vector.tensor_copy if by_vector else nc.scalar.copy
-                    copy(
-                        out=grouped[:, e * BANK : (e + 1) * BANK].rearrange(
-                            "p (g q u) -> p g q u", g=PASSES, u=PAIR
-                        ),
-                        in_=flipped[:].rearrange("p (g u q) -> p g q u", g=PASSES, u=PAIR),
-                    )
+
+            def empty_bank(n, e):
+                if e == 0:
+                    grouped[n] = stage.tile([P, PAIR * BANK], F32, align_bytes=64, name="grouped")
+                by_vector = slabs[n][2] == CANDIDATE and e == PAIR - 1
+                copy = nc.vector.tensor_copy if by_vector else nc.scalar.copy
+                copy(
+                    out=grouped[n][:, e * BANK : (e + 1) * BANK].rearrange(
+                        "p (g q u) -> p g q u", g=PASSES, u=PAIR
+                    ),
+                    in_=flipped[(n, e)][:].rearrange("p (g u q) -> p g q u", g=PASSES, u=PAIR),
+                )
+
+            def quantise_slab(n):
                 nc.vector.quantize_mx(
-                    out=w_codes[slab][:].bitcast(FP8X4),
-                    scales=w_scales[slab][:],
-                    in_=grouped[:].bitcast(BF16),
+                    out=w_codes[n][:].bitcast(FP8X4),
+                    scales=w_scales[n][:],
+                    in_=grouped[n][:].bitcast(BF16),
                 )
 
-            def first_level(side, blk):
-                rounds = gru_round(side, blk, x_codes, x_scales, [x_f32[:, blk, :, :]], sums1, work1)
-                diff, cand = rounds[0]
-                nc.vector.tensor_add(out=c_f32[(side, blk)][:], in0=diff[:], in1=cand)
-                g, u = divmod(blk, PAIR)
-                nc.vector.tensor_copy(
-                    out=c_grouped[g][:, side * ROOTS : (side + 1) * ROOTS, u * PAIR : (u + 1) * PAIR],
-                    in_=c_f32[(side, blk)][:].rearrange("p e j -> p j e"),
-                )
-                if u == PAIR - 1 and side == SIDES - 1:
-                    nc.vector.quantize_mx(
-                        out=c_codes[g][:].bitcast(FP8X4),
-                        scales=c_scales[g][:],
-                        in_=c_grouped[g][:].rearrange("p c t -> p (c t)"),
-                    )
+            def multiply_slab(n):
+                sums[n] = gates1.tile([P, PAIR, ROOTS], F32, name="sums")
+                multiply(sums[n], n, x_codes, x_scales)
 
-            for i, (side, blk) in enumerate(blocks):
-                for gate in range(GATES):
-                    quantise_slab((side, blk, gate))
-                if i > 0:
-                    first_level(*blocks[i - 1])
-            first_level(*blocks[-1])
+            def slab_behind(n, lag):
+                m = n - lag
+                if 0 <= m < SLABS:
+                    return (m,) + slabs[m]
+                return (m, None, None, None)
+
+            def activate(n, e):
+                m, blk, side, gate = slab_behind(n, MULTIPLY_LAG)
+                if gate == RESET or gate == UPDATE:
+                    gate_out = reset if gate == RESET else update
+                    if e == 0:
+                        gate_out[m // GATES] = work1.tile(
+                            [P, PAIR, ROOTS], F32, name="reset" if gate == RESET else "update"
+                        )
+                    sigmoid(gate_out[m // GATES], sums[m], side, gate, blk, e)
+                m, blk, side, gate = slab_behind(n, TANH_LAG)
+                if gate == CANDIDATE:
+                    tanh(cand[m // GATES], side, blk, e)
+
+            def vector_share(n, half):
+                m, blk, side, gate = slab_behind(n, MULTIPLY_LAG)
+                if gate == CANDIDATE:
+                    i = m // GATES
+                    if half == 0:
+                        cand[i] = work1.tile([P, PAIR, ROOTS], F32, name="cand")
+                    reset_candidate(cand[i], sums[m], reset[i], side, blk, half)
+                m, blk, side, gate = slab_behind(n, MIX_LAG)
+                if gate == CANDIDATE:
+                    i = m // GATES
+                    if half == 0:
+                        diff[i] = work1.tile([P, PAIR, ROOTS], F32, name="diff")
+                        nc.vector.tensor_sub(out=diff[i][:], in0=x_f32[:, blk, :, :], in1=cand[i][:])
+                    else:
+                        nc.vector.tensor_mul(out=diff[i][:], in0=update[i][:], in1=diff[i][:])
+                m, blk, side, gate = slab_behind(n, SUM_LAG)
+                if gate == CANDIDATE:
+                    i = m // GATES
+                    nodes = slice(side * ROOTS, (side + 1) * ROOTS)
+                    g, u = divmod(blk, PAIR)
+                    if half == 0:
+                        nc.vector.tensor_add(
+                            out=c_grouped[g][:, nodes, u * PAIR : (u + 1) * PAIR],
+                            in0=diff[i][:].rearrange("p e j -> p j e"),
+                            in1=cand[i][:].rearrange("p e j -> p j e"),
+                        )
+                    else:
+                        nc.vector.tensor_add(
+                            out=c_f32[blk][:, :, nodes], in0=diff[i][:], in1=cand[i][:]
+                        )
+                        if u == PAIR - 1 and side == SIDES - 1:
+                            nc.vector.quantize_mx(
+                                out=c_codes[g][:].bitcast(FP8X4),
+                                scales=c_scales[g][:],
+                                in_=c_grouped[g][:].rearrange("p c t -> p (c t)"),
+                            )
+
+            for first in range(0, SLABS + SUM_LAG + 1, RUN):
+                steps = range(first, first + RUN)
+                for n in steps:
+                    if n < SLABS:
+                        transpose_slab(n)
+                for n in steps:
+                    if 0 <= n - MULTIPLY_LAG < SLABS:
+                        multiply_slab(n - MULTIPLY_LAG)
+                for n in steps:
+                    vector_share(n, 0)
+                    if 0 <= n - 1 < SLABS:
+                        quantise_slab(n - 1)
+                    vector_share(n, 1)
+                    for e in range(PAIR):
+                        if n < SLABS:
+                            empty_bank(n, e)
+                        activate(n, e)
 
         with tc.tile_pool(name="work2", bufs=4) as work2, tc.psum_pool(
-            name="sums2", bufs=6
-        ) as sums2, tc.psum_pool(name="back", bufs=2) as back_psum:
-            for side2, blk in blocks:
-                rounds = gru_round(
-                    side2, blk, c_codes, c_scales, [c_f32[(s, blk)][:] for s in range(SIDES)],
-                    sums2, work2,
-                )
-                back = back_psum.tile([P, SIDES, PAIR, P], F32)
-                for s, (diff, cand) in enumerate(rounds):
-                    nc.vector.tensor_add(out=diff[:], in0=diff[:], in1=cand)
+            name="gates2", bufs=2
+        ) as gates2, tc.psum_pool(name="back", bufs=2) as back_psum:
+            children = SIDES * ROOTS
+            blocks2 = [(side2, blk) for side2 in range(SIDES) for blk in range(BLOCKS)]
+            update2, cand2, mixed, back = {}, {}, {}, {}
+
+            def gates_of_block(k):
+                side2, blk = blocks2[k]
+                banks = []
+                for gate in range(GATES):
+                    bank = gates2.tile([P, PAIR, children], F32, name="sums%d" % gate)
+                    multiply(bank, slab_index(blk, side2, gate), c_codes, c_scales)
+                    banks.append(bank)
+                return banks
+
+            def activate_block(k, banks):
+                side2, blk = blocks2[k]
+                reset2 = work2.tile([P, PAIR, children], F32)
+                update2[k] = work2.tile([P, PAIR, children], F32, name="update2")
+                cand2[k] = work2.tile([P, PAIR, children], F32, name="cand2")
+                for e in range(PAIR):
+                    sigmoid(reset2, banks[RESET], side2, RESET, blk, e)
+                if k >= 1:
+                    mix_begin(k - 1)
+                for e in range(PAIR):
+                    reset_candidate(cand2[k], banks[CANDIDATE], reset2, side2, blk, e)
+                for e in range(PAIR):
+                    sigmoid(update2[k], banks[UPDATE], side2, UPDATE, blk, e)
+                for e in range(PAIR):
+                    tanh(cand2[k], side2, blk, e)
+
+            def mix_begin(k):
+                side2, blk = blocks2[k]
+                mixed[k] = work2.tile([P, PAIR, children], F32, name="mixed")
+                for e in range(PAIR):
+                    nc.vector.tensor_sub(
+                        out=mixed[k][:, e, :], in0=c_f32[blk][:, e, :], in1=cand2[k][:, e, :]
+                    )
+
+            def mix_end(k):
+                for e in range(PAIR):
+                    nc.vector.tensor_mul(
+                        out=mixed[k][:, e, :], in0=update2[k][:, e, :], in1=mixed[k][:, e, :]
+                    )
+                for e in range(PAIR):
+                    nc.vector.tensor_add(
+                        out=mixed[k][:, e, :], in0=mixed[k][:, e, :], in1=cand2[k][:, e, :]
+                    )
+
+            def transpose_back(k):
+                back[k] = back_psum.tile([P, SIDES, PAIR, P], F32, name="back")
+                for s in range(SIDES):
                     for e in range(PAIR):
-                        nc.tensor.transpose(back[:, s, e, :], diff[:, e, :], identity[:])
+                        nc.tensor.transpose(
+                            back[k][:, s, e, :], mixed[k][:, e, s * ROOTS : (s + 1) * ROOTS], identity[:]
+                        )
+
+            def store_block(k):
+                side2, blk = blocks2[k]
+                cols = slice(blk * BLOCK, (blk + 1) * BLOCK)
                 leaving = work2.tile([P, SIDES, BLOCK], F32)
                 nc.scalar.copy(
                     out=leaving[:].rearrange("j s (q e) -> j s q e", e=PAIR),
-                    in_=back[:].rearrange("j s e q -> j s q e"),
+                    in_=back[k][:].rearrange("j s e q -> j s q e"),
                 )
-                cols = slice(blk * BLOCK, (blk + 1) * BLOCK)
                 nc.sync.dma_start(out=out_rows[:, :, side2, cols], in_=leaving[:])
+
+            count = len(blocks2)
+            for k in range(count + 3):
+                if k < count:
+                    banks = gates_of_block(k)
+                if k >= 3:
+                    transpose_back(k - 3)
+                if k < count:
+                    activate_block(k, banks)
+                elif k == count:
+                    mix_begin(k - 1)
+                if 1 <= k <= count:
+                    mix_end(k - 1)
+                if k >= 3:
+                    store_block(k - 3)

import concourse.mybir as mybir
from concourse.masks import make_identity

F32 = mybir.dt.float32
BF16 = mybir.dt.bfloat16
U32 = mybir.dt.uint32
U8 = mybir.dt.uint8
FP8X4 = mybir.dt.float8_e4m3fn_x4
ACT = mybir.ActivationFunctionType
ALU = mybir.AluOpType

P = 128
H = 1024
GATES = 3
RESET, UPDATE, CANDIDATE = 0, 1, 2
LOAD_ORDER = [RESET, CANDIDATE, UPDATE]
SIDES = 2
PAIR = 2
ROOTS = 128
BLOCK = P * PAIR
BLOCKS = H // BLOCK
PASSES = H // (4 * P)
WORD_BLOCKS = H // BLOCK
BANK = 512
SLABS = SIDES * BLOCKS * GATES
SLAB_WORDS = PAIR * PASSES * P

MULTIPLY_LAG = 3
TANH_LAG = 6
MIX_LAG = 7
SUM_LAG = 8
RUN = 2

FLOPS = 2 * (ROOTS + SIDES * ROOTS) * (SIDES * GATES * H) * H


def tile_decodertreernn_pa_kernel(
    tc, h_nodes, Whh_l, bih_l, bhh_l, Whh_r, bih_r, bhh_r, out
):
    nc = tc.nc

    slab_rows = [
        w.rearrange("(gate blk q e) k -> gate blk q (e k)", gate=GATES, blk=BLOCKS, q=P, e=PAIR)
        for w in (Whh_l, Whh_r)
    ]
    out_rows = out.rearrange("b (i s s2) h -> (b i) s s2 h", s=SIDES, s2=SIDES)

    slabs = [
        (blk, side, gate)
        for blk in range(BLOCKS)
        for side in range(SIDES)
        for gate in LOAD_ORDER
    ]

    def slab_index(blk, side, gate):
        return (blk * SIDES + side) * GATES + LOAD_ORDER.index(gate)

    with tc.manual_schedule(), tc.tile_pool(name="keep", bufs=1) as keep:
        identity = keep.tile([P, P], F32)
        make_identity(nc, identity[:])

        w_codes = [
            keep.tile([P, SLAB_WORDS], U32, align_bytes=64, name="w_codes%d" % n) for n in range(SLABS)
        ]
        w_scales = [
            keep.tile([P, SLAB_WORDS], U8, align_bytes=64, name="w_scales%d" % n) for n in range(SLABS)
        ]
        x_codes = [
            keep.tile([P, ROOTS], U32, align_bytes=64, name="x_codes%d" % g) for g in range(PASSES)
        ]
        x_scales = [
            keep.tile([P, ROOTS], U8, align_bytes=64, name="x_scales%d" % g) for g in range(PASSES)
        ]
        c_codes = [
            keep.tile([P, SIDES * ROOTS], U32, align_bytes=64, name="c_codes%d" % g)
            for g in range(PASSES)
        ]
        c_scales = [
            keep.tile([P, SIDES * ROOTS], U8, align_bytes=64, name="c_scales%d" % g)
            for g in range(PASSES)
        ]
        x_f32 = keep.tile([P, BLOCKS, PAIR, ROOTS], F32)
        c_f32 = [
            keep.tile([P, PAIR, SIDES * ROOTS], F32, name="c_f32_%d" % blk) for blk in range(BLOCKS)
        ]
        c_grouped = [
            keep.tile([P, SIDES * ROOTS, 2 * PAIR], BF16, align_bytes=64, name="c_grouped%d" % g)
            for g in range(PASSES)
        ]
        bias = keep.tile([P, SIDES * 2 * GATES * BLOCKS * PAIR], F32)
        bias_rz = keep.tile([P, SIDES, 2 * BLOCKS * PAIR], F32)

        def bias_column(side, kind, gate, blk, e):
            col = ((side * 2 + kind) * GATES * BLOCKS + gate * BLOCKS + blk) * PAIR + e
            return bias[:, col : col + 1]

        def bias_rz_column(side, gate, blk, e):
            col = (gate * BLOCKS + blk) * PAIR + e
            return bias_rz[:, side, col : col + 1]

        def multiply(bank, slab, codes, scales):
            for e in range(PAIR):
                for g in range(PASSES):
                    first = (e * PASSES + g) * P
                    nc.tensor.matmul_mx(
                        out=bank[:, e, :],
                        lhsT=w_codes[slab][:, first : first + P].bitcast(FP8X4),
                        lhsT_scale=w_scales[slab][:, first : first + P],
                        rhs=codes[g][:].bitcast(FP8X4),
                        rhs_scale=scales[g][:],
                        start=(g == 0),
                        stop=(g == PASSES - 1),
                    )

        def sigmoid(gate_out, bank, side, gate, blk, e):
            nc.scalar.activation(
                out=gate_out[:, e, :], in_=bank[:, e, :], func=ACT.Sigmoid,
                bias=bias_rz_column(side, gate, blk, e), scale=1.0,
            )

        def reset_candidate(cand, bank, reset, side, blk, e):
            nc.vector.scalar_tensor_tensor(
                out=cand[:, e, :], in0=bank[:, e, :], scalar=bias_column(side, 1, CANDIDATE, blk, e),
                in1=reset[:, e, :], op0=ALU.add, op1=ALU.mult,
            )

        def tanh(cand, side, blk, e):
            nc.scalar.activation(
                out=cand[:, e, :], in_=cand[:, e, :], func=ACT.Tanh,
                bias=bias_column(side, 0, CANDIDATE, blk, e), scale=1.0,
            )

        with tc.tile_pool(name="raw", bufs=SLABS) as raw_pool, tc.tile_pool(
            name="once", bufs=1
        ) as once, tc.tile_pool(name="stage", bufs=4) as stage, tc.tile_pool(
            name="work1", bufs=3
        ) as work1, tc.psum_pool(name="flip", bufs=5) as flip_psum, tc.psum_pool(
            name="gates1", bufs=3
        ) as gates1:
            x_raw = once.tile([P, H], BF16)
            nc.sync.dma_start(out=x_raw[:], in_=h_nodes.flatten_outer_dims())
            raw = []
            for blk, side, gate in slabs:
                raw_slab = raw_pool.tile([P, PAIR * H], BF16, name="raw_slab")
                nc.sync.dma_start(out=raw_slab[:], in_=slab_rows[side][gate, blk])
                raw.append(raw_slab)
            bias_raw = once.tile([P, BLOCK], BF16)
            nc.vector.memset(bias_raw[:], 0.0)
            for v, vec in enumerate((bih_l, bhh_l, bih_r, bhh_r)):
                rows = GATES * BLOCKS
                nc.scalar.dma_start(
                    out=bias_raw[v * rows : (v + 1) * rows, :],
                    in_=vec.rearrange("(r c) -> r c", c=BLOCK),
                )

            warm = once.tile([P, 1], F32)
            nc.vector.memset(warm[:], 0.0)
            nc.scalar.activation(out=warm[:], in_=warm[:], func=ACT.Sigmoid)

            x_words = x_raw[:].bitcast(F32)
            x_flipped = flip_psum.tile([P, BANK], F32, name="flipped")
            for w in range(WORD_BLOCKS):
                nc.tensor.transpose(
                    x_flipped[:, w * P : (w + 1) * P], x_words[:, w * P : (w + 1) * P], identity[:]
                )
            x_grouped = once.tile([P, BANK], F32, align_bytes=64)
            nc.vector.tensor_copy(
                out=x_grouped[:].rearrange("p (g j u) -> p g j u", g=PASSES, u=PAIR),
                in_=x_flipped[:].rearrange("p (g u j) -> p g j u", g=PASSES, u=PAIR),
            )
            nc.scalar.copy(
                out=x_f32[:],
                in_=x_flipped[:].bitcast(BF16).rearrange(
                    "p (blk j e) -> p blk e j", blk=BLOCKS, e=PAIR
                ),
            )

            b_flipped = flip_psum.tile([P, BANK], F32, name="flipped")
            nc.tensor.transpose(b_flipped[:, 0:P], bias_raw[:].bitcast(F32), identity[:])
            bias_words = SIDES * 2 * GATES * BLOCKS
            nc.vector.tensor_copy(out=bias[:], in_=b_flipped[:, 0:bias_words].bitcast(BF16))
            by_kind = bias[:].rearrange("p (s kind c) -> p s kind c", s=SIDES, kind=2)
            rz_cols = 2 * BLOCKS * PAIR
            nc.vector.tensor_add(
                out=bias_rz[:], in0=by_kind[:, :, 0, 0:rz_cols], in1=by_kind[:, :, 1, 0:rz_cols]
            )
            for g in range(PASSES):
                nc.vector.quantize_mx(
                    out=x_codes[g][:].bitcast(FP8X4),
                    scales=x_scales[g][:],
                    in_=x_grouped[:, g * BLOCK : (g + 1) * BLOCK].bitcast(BF16),
                )

            flipped = {}
            grouped = {}
            sums = {}
            reset, update, cand, diff = {}, {}, {}, {}

            def transpose_slab(n):
                words = raw[n][:].bitcast(F32)
                for e in range(PAIR):
                    flipped[(n, e)] = flip_psum.tile([P, BANK], F32, name="flipped")
                    for w in range(WORD_BLOCKS):
                        first = (e * WORD_BLOCKS + w) * P
                        nc.tensor.transpose(
                            flipped[(n, e)][:, w * P : (w + 1) * P],
                            words[:, first : first + P],
                            identity[:],
                        )

            def empty_bank(n, e):
                if e == 0:
                    grouped[n] = stage.tile([P, PAIR * BANK], F32, align_bytes=64, name="grouped")
                by_vector = slabs[n][2] == CANDIDATE and e == PAIR - 1
                copy = nc.vector.tensor_copy if by_vector else nc.scalar.copy
                copy(
                    out=grouped[n][:, e * BANK : (e + 1) * BANK].rearrange(
                        "p (g q u) -> p g q u", g=PASSES, u=PAIR
                    ),
                    in_=flipped[(n, e)][:].rearrange("p (g u q) -> p g q u", g=PASSES, u=PAIR),
                )

            def quantise_slab(n):
                nc.vector.quantize_mx(
                    out=w_codes[n][:].bitcast(FP8X4),
                    scales=w_scales[n][:],
                    in_=grouped[n][:].bitcast(BF16),
                )

            def multiply_slab(n):
                sums[n] = gates1.tile([P, PAIR, ROOTS], F32, name="sums")
                multiply(sums[n], n, x_codes, x_scales)

            def slab_behind(n, lag):
                m = n - lag
                if 0 <= m < SLABS:
                    return (m,) + slabs[m]
                return (m, None, None, None)

            def activate(n, e):
                m, blk, side, gate = slab_behind(n, MULTIPLY_LAG)
                if gate == RESET or gate == UPDATE:
                    gate_out = reset if gate == RESET else update
                    if e == 0:
                        gate_out[m // GATES] = work1.tile(
                            [P, PAIR, ROOTS], F32, name="reset" if gate == RESET else "update"
                        )
                    sigmoid(gate_out[m // GATES], sums[m], side, gate, blk, e)
                m, blk, side, gate = slab_behind(n, TANH_LAG)
                if gate == CANDIDATE:
                    tanh(cand[m // GATES], side, blk, e)

            def vector_share(n, half):
                m, blk, side, gate = slab_behind(n, MULTIPLY_LAG)
                if gate == CANDIDATE:
                    i = m // GATES
                    if half == 0:
                        cand[i] = work1.tile([P, PAIR, ROOTS], F32, name="cand")
                    reset_candidate(cand[i], sums[m], reset[i], side, blk, half)
                m, blk, side, gate = slab_behind(n, MIX_LAG)
                if gate == CANDIDATE:
                    i = m // GATES
                    if half == 0:
                        diff[i] = work1.tile([P, PAIR, ROOTS], F32, name="diff")
                        nc.vector.tensor_sub(out=diff[i][:], in0=x_f32[:, blk, :, :], in1=cand[i][:])
                    else:
                        nc.vector.tensor_mul(out=diff[i][:], in0=update[i][:], in1=diff[i][:])
                m, blk, side, gate = slab_behind(n, SUM_LAG)
                if gate == CANDIDATE:
                    i = m // GATES
                    nodes = slice(side * ROOTS, (side + 1) * ROOTS)
                    g, u = divmod(blk, PAIR)
                    if half == 0:
                        nc.vector.tensor_add(
                            out=c_grouped[g][:, nodes, u * PAIR : (u + 1) * PAIR],
                            in0=diff[i][:].rearrange("p e j -> p j e"),
                            in1=cand[i][:].rearrange("p e j -> p j e"),
                        )
                    else:
                        nc.vector.tensor_add(
                            out=c_f32[blk][:, :, nodes], in0=diff[i][:], in1=cand[i][:]
                        )
                        if u == PAIR - 1 and side == SIDES - 1:
                            nc.vector.quantize_mx(
                                out=c_codes[g][:].bitcast(FP8X4),
                                scales=c_scales[g][:],
                                in_=c_grouped[g][:].rearrange("p c t -> p (c t)"),
                            )

            for first in range(0, SLABS + SUM_LAG + 1, RUN):
                steps = range(first, first + RUN)
                for n in steps:
                    if n < SLABS:
                        transpose_slab(n)
                for n in steps:
                    if 0 <= n - MULTIPLY_LAG < SLABS:
                        multiply_slab(n - MULTIPLY_LAG)
                for n in steps:
                    vector_share(n, 0)
                    if 0 <= n - 1 < SLABS:
                        quantise_slab(n - 1)
                    vector_share(n, 1)
                    for e in range(PAIR):
                        if n < SLABS:
                            empty_bank(n, e)
                        activate(n, e)

        with tc.tile_pool(name="work2", bufs=4) as work2, tc.psum_pool(
            name="gates2", bufs=2
        ) as gates2, tc.psum_pool(name="back", bufs=2) as back_psum:
            children = SIDES * ROOTS
            blocks2 = [(side2, blk) for side2 in range(SIDES) for blk in range(BLOCKS)]
            update2, cand2, mixed, back = {}, {}, {}, {}

            def gates_of_block(k):
                side2, blk = blocks2[k]
                banks = []
                for gate in range(GATES):
                    bank = gates2.tile([P, PAIR, children], F32, name="sums%d" % gate)
                    multiply(bank, slab_index(blk, side2, gate), c_codes, c_scales)
                    banks.append(bank)
                return banks

            def activate_block(k, banks):
                side2, blk = blocks2[k]
                reset2 = work2.tile([P, PAIR, children], F32)
                update2[k] = work2.tile([P, PAIR, children], F32, name="update2")
                cand2[k] = work2.tile([P, PAIR, children], F32, name="cand2")
                for e in range(PAIR):
                    sigmoid(reset2, banks[RESET], side2, RESET, blk, e)
                if k >= 1:
                    mix_begin(k - 1)
                for e in range(PAIR):
                    reset_candidate(cand2[k], banks[CANDIDATE], reset2, side2, blk, e)
                for e in range(PAIR):
                    sigmoid(update2[k], banks[UPDATE], side2, UPDATE, blk, e)
                for e in range(PAIR):
                    tanh(cand2[k], side2, blk, e)

            def mix_begin(k):
                side2, blk = blocks2[k]
                mixed[k] = work2.tile([P, PAIR, children], F32, name="mixed")
                for e in range(PAIR):
                    nc.vector.tensor_sub(
                        out=mixed[k][:, e, :], in0=c_f32[blk][:, e, :], in1=cand2[k][:, e, :]
                    )

            def mix_end(k):
                for e in range(PAIR):
                    nc.vector.tensor_mul(
                        out=mixed[k][:, e, :], in0=update2[k][:, e, :], in1=mixed[k][:, e, :]
                    )
                for e in range(PAIR):
                    nc.vector.tensor_add(
                        out=mixed[k][:, e, :], in0=mixed[k][:, e, :], in1=cand2[k][:, e, :]
                    )

            def transpose_back(k):
                back[k] = back_psum.tile([P, SIDES, PAIR, P], F32, name="back")
                for s in range(SIDES):
                    for e in range(PAIR):
                        nc.tensor.transpose(
                            back[k][:, s, e, :], mixed[k][:, e, s * ROOTS : (s + 1) * ROOTS], identity[:]
                        )

            def store_block(k):
                side2, blk = blocks2[k]
                cols = slice(blk * BLOCK, (blk + 1) * BLOCK)
                leaving = work2.tile([P, SIDES, BLOCK], F32)
                nc.scalar.copy(
                    out=leaving[:].rearrange("j s (q e) -> j s q e", e=PAIR),
                    in_=back[k][:].rearrange("j s e q -> j s q e"),
                )
                nc.sync.dma_start(out=out_rows[:, :, side2, cols], in_=leaving[:])

            count = len(blocks2)
            for k in range(count + 3):
                if k < count:
                    banks = gates_of_block(k)
                if k >= 3:
                    transpose_back(k - 3)
                if k < count:
                    activate_block(k, banks)
                elif k == count:
                    mix_begin(k - 1)
                if 1 <= k <= count:
                    mix_end(k - 1)
                if k >= 3:
                    store_block(k - 3)
